import numpy as np
import ml_dtypes


def mxq(x, axis, fmt="e4m3"):
    dtype, down = {"e4m3": (ml_dtypes.float8_e4m3fn, 7), "e5m2": (ml_dtypes.float8_e5m2, 14)}[fmt]
    v = np.moveaxis(np.asarray(x, np.float32).astype(ml_dtypes.bfloat16).astype(np.float64), axis, -1)
    blocks = v.reshape(v.shape[:-1] + (-1, 32))
    amax = np.abs(blocks).max(-1, keepdims=True)
    byte = np.maximum(np.where(amax > 0, np.frexp(amax)[1] - 1 + 127, 0) - down, 1)
    scale = np.exp2(byte - 127.0)
    codes = (blocks / scale).astype(np.float32).astype(dtype).astype(np.float64)
    return np.moveaxis((codes * scale).reshape(v.shape), -1, axis)


WIDE = False


def mx_kscale(k):
    if not WIDE:
        return np.ones(k)
    levels = np.array([10, -10, 5, -5, 0])
    a = np.random.permutation(np.resize(levels, k // 512 * 4)).reshape(k // 512, 4)
    idx = np.arange(k)
    return np.exp2(a[idx // 512, idx % 128 // 32])


BF16 = ml_dtypes.bfloat16


def bf(x):
    return np.asarray(x, np.float32).astype(BF16)


def f64(x):
    return np.asarray(x).astype(np.float64)


S, P, B, E, H, I = 128, 384, 4, 1024, 16, 64
J = P + S
HI = H * I
SCALE = 1.0 / np.sqrt(I)
LN_EPS = 1e-5


def rel_shift(x):
    b, h, s, j = x.shape
    padded = np.concatenate([np.zeros((b, h, s, 1)), x], axis=3)
    return padded.reshape(b, h, j + 1, s)[:, :, 1:].reshape(b, h, s, j)


def setup_inputs():
    t = mx_kscale(HI)
    return {
        "content_scores": bf(np.random.standard_normal((B, H, S, J)) * np.sqrt(I)),
        "pos_scores": bf(np.random.standard_normal((B, H, S, J)) * np.sqrt(I)),
        "values": bf(np.random.standard_normal((B, H, J, I)) * t.reshape(1, H, 1, I)),
        "mask": np.triu(np.ones((S, J), bool), k=1 + P),
        "inputMHA": bf(np.random.standard_normal((S, B, E))),
        "W_out": bf(np.random.standard_normal((E, HI)) * 5.0 / np.sqrt(HI) / t[None, :]),
        "ln_w": bf(1.0 + 0.1 * np.random.standard_normal(E)),
        "ln_b": bf(0.1 * np.random.standard_normal(E)),
    }


def reference(content_scores, pos_scores, values, mask, inputMHA, W_out, ln_w, ln_b):
    a = f64(content_scores) + rel_shift(f64(pos_scores))
    a = np.where(f64(mask) > 0.5, -np.inf, a) * SCALE
    e = np.exp(a - a.max(-1, keepdims=True))
    ctx = (mxq(e, 3, "e4m3") @ mxq(f64(values), 2, "e4m3")) / e.sum(-1, keepdims=True)
    c = ctx.transpose(2, 0, 1, 3).reshape(S, B, HI)
    o = f64(inputMHA) + (mxq(c, 2, "e4m3") @ mxq(f64(W_out), 1, "e4m3").T)
    mu = o.mean(-1, keepdims=True)
    var = ((o - mu) ** 2).mean(-1, keepdims=True)
    return (o - mu) / np.sqrt(var + LN_EPS) * f64(ln_w) + f64(ln_b)

@@ -1,0 +1,376 @@
+from contextlib import ExitStack
+
+import concourse.mybir as mybir
+from concourse.masks import make_identity
+
+BF16 = mybir.dt.bfloat16
+F32 = mybir.dt.float32
+I32 = mybir.dt.int32
+U32 = mybir.dt.uint32
+U8 = mybir.dt.uint8
+FP8X4 = mybir.dt.float8_e4m3fn_x4
+ALU = mybir.AluOpType
+ACT = mybir.ActivationFunctionType
+AXIS_X = mybir.AxisListType.X
+
+P = 128
+BATCH = 4
+HEADS = 16
+KEYS = 512
+WIDTH = 64
+FEATURES = HEADS * WIDTH
+ALL_HEADS = BATCH * HEADS
+PACK = 4
+K_PASS = P * PACK
+WORDS = K_PASS // 2
+PASSES = FEATURES // K_PASS
+N_TILE = 512
+SCALE = 0.125
+LN_EPS = 1e-5
+WINDOW = P
+OPEN_KEYS = KEYS - WINDOW
+HIDDEN = 1e30
+
+GROUP = 4
+POOL_HEADS = 3
+VECTOR_HEADS = GROUP - POOL_HEADS
+GROUPS = ALL_HEADS // GROUP
+GROUPS_PER_BATCH = HEADS // GROUP
+BANK_HEADS = N_TILE // WIDTH
+BANK_GROUPS = BANK_HEADS // GROUP
+SCORE_BUFS = 4
+W_ROWS = FEATURES // P
+W_FIRST_STEP = 3
+W_PER_STEP = 2
+
+FLOPS = 2 * ALL_HEADS * P * KEYS * WIDTH + 2 * BATCH * P * FEATURES * FEATURES
+
+
+def tile_maskedmultiheadattention_pa_kernel(
+    tc, content_scores, pos_scores, values, mask, inputMHA, W_out, ln_w, ln_b, out
+):
+    nc = tc.nc
+    with ExitStack() as ctx:
+        ctx.enter_context(tc.manual_schedule())
+        const = ctx.enter_context(tc.tile_pool(name="const", bufs=1))
+        scores_in = ctx.enter_context(tc.tile_pool(name="scores_in", bufs=SCORE_BUFS))
+        triple = ctx.enter_context(tc.tile_pool(name="triple", bufs=3))
+        double = ctx.enter_context(tc.tile_pool(name="double", bufs=2))
+        psum = ctx.enter_context(tc.psum_pool(name="psum", bufs=2))
+
+        content_view = content_scores.rearrange("b h s j -> s (b h) j")
+        pos_flat = pos_scores.rearrange("b h s j -> (b h) (s j)")
+        skew = KEYS - 1
+        pos_from_0 = pos_flat[:, P - 1 : P - 1 + P * skew].rearrange("n (s j) -> s n j", j=skew)
+        pos_from_1 = pos_flat[:, P : P + P * skew].rearrange("n (s j) -> s n j", j=skew)
+        values_view = values.rearrange("b h (u p w) i -> p (b h u) (w i)", u=2, p=P, w=2)
+        w_view = W_out.rearrange("(r p) f -> p r f", p=P)
+
+        identity = const.tile([P, P], F32)
+        make_identity(nc, identity[:])
+        minus_half = const.tile([P, 1], F32)
+        nc.vector.memset(minus_half[:], -0.5)
+        table_warmer = const.tile([P, 1], F32)
+        nc.scalar.activation(out=table_warmer[:], in_=minus_half[:], func=ACT.Exp)
+
+        mask_words = const.tile([P, WINDOW, 2], I32)
+        nc.sync.dma_start(
+            out=mask_words[:].rearrange("p j w -> p (j w)"), in_=mask.bitcast(I32)[:, 2 * OPEN_KEYS : 2 * KEYS]
+        )
+        cap = const.tile([P, WINDOW], BF16)
+        nc.vector.tensor_scalar(
+            out=cap[:], in0=mask_words[:, :, 0], scalar1=-2.0 * HIDDEN, scalar2=HIDDEN, op0=ALU.mult, op1=ALU.add
+        )
+
+        rowsum = const.tile([P, ALL_HEADS], F32)
+        v_codes = const.tile([P, ALL_HEADS * WIDTH], U32, align_bytes=64)
+        v_scales = const.tile([P, ALL_HEADS * WIDTH], U8, align_bytes=64)
+        w_raw = const.tile([P, W_ROWS, FEATURES], BF16)
+        w_codes = const.tile([P, PASSES, FEATURES], U32, align_bytes=64)
+        w_scales = const.tile([P, PASSES, FEATURES], U8, align_bytes=64)
+        residual = const.tile([P, BATCH, FEATURES], BF16)
+        gain = const.tile([P, FEATURES], BF16)
+        bias = const.tile([P, FEATURES], BF16)
+
+        content_of, pos_of, v_raw_of = {}, {}, {}
+        sum_of, top_of, shift_of, e_grouped_of, e_codes_of, e_scales_of, v_grouped_of = {}, {}, {}, {}, {}, {}, {}
+        w_grouped_of, ctx_bank_of, inverse_of, c_of, c_words_of, c_grouped_of, o_banks_of, o_of, moments_of, rstd_of = (
+            {}, {}, {}, {}, {}, {}, {}, {}, {}, {},
+        )
+
+        def load_scores(g):
+            heads = slice(g * GROUP, (g + 1) * GROUP)
+            content_of[g] = scores_in.tile([P, GROUP, KEYS], BF16, name="content")
+            nc.sync.dma_start(out=content_of[g][:], in_=content_view[:, heads, :])
+            pos_of[g] = scores_in.tile([P, GROUP, KEYS], BF16, name="pos")
+            nc.sync.dma_start(out=pos_of[g][:, :, 0:OPEN_KEYS], in_=pos_from_0[:, heads, 0:OPEN_KEYS])
+            nc.sync.dma_start(out=pos_of[g][:, :, OPEN_KEYS:KEYS], in_=pos_from_1[:, heads, OPEN_KEYS - 1 : KEYS - 1])
+
+        def load_values(b):
+            v_raw_of[b] = double.tile([P, HEADS, PACK, WIDTH], BF16, name="v_raw")
+            nc.sync.dma_start(
+                out=v_raw_of[b][:].rearrange("p n (u w) i -> p (n u) (w i)", u=2),
+                in_=values_view[:, b * HEADS * 2 : (b + 1) * HEADS * 2, :],
+            )
+
+        def hide(g):
+            window = pos_of[g][:, :, OPEN_KEYS:KEYS]
+            nc.vector.tensor_tensor(
+                out=window, in0=window, in1=cap[:].unsqueeze(1).to_broadcast([P, GROUP, WINDOW]), op=ALU.min
+            )
+            sum_of[g] = triple.tile([P, GROUP, KEYS], F32, name="score_sum")
+            nc.gpsimd.tensor_tensor(
+                out=sum_of[g][:, VECTOR_HEADS:GROUP, :],
+                in0=content_of[g][:, VECTOR_HEADS:GROUP, :],
+                in1=pos_of[g][:, VECTOR_HEADS:GROUP, :],
+                op=ALU.add,
+            )
+
+        def add_scores(g):
+            nc.vector.tensor_tensor(
+                out=sum_of[g][:, 0:VECTOR_HEADS, :],
+                in0=content_of[g][:, 0:VECTOR_HEADS, :],
+                in1=pos_of[g][:, 0:VECTOR_HEADS, :],
+                op=ALU.add,
+            )
+
+        def row_maxima(g):
+            top_of[g] = triple.tile([P, GROUP], F32, name="top")
+            nc.vector.tensor_reduce(out=top_of[g][:], in_=sum_of[g][:], axis=AXIS_X, op=ALU.max)
+
+        def shifts(g):
+            shift_of[g] = triple.tile([P, GROUP], F32, name="shift")
+            nc.vector.tensor_scalar_mul(out=shift_of[g][:], in0=top_of[g][:], scalar1=-SCALE)
+
+        def exponentials(g):
+            e = double.tile([P, GROUP, KEYS], BF16, name="e")
+            for k in range(GROUP):
+                n = g * GROUP + k
+                nc.scalar.activation(
+                    out=e[:, k, :],
+                    in_=sum_of[g][:, k, :],
+                    func=ACT.Exp,
+                    bias=shift_of[g][:, k : k + 1],
+                    scale=SCALE,
+                    accum_out=rowsum[:, n : n + 1],
+                )
+            e_grouped_of[g] = triple.tile([P, GROUP, P, PACK], BF16, name="e_grouped", align_bytes=64)
+            for pair in range(GROUP // 2):
+                e_t = psum.tile([P, 2, 2, P], F32, name="e_t")
+                for k in range(2):
+                    e_words = e[:, 2 * pair + k, :].bitcast(F32)
+                    for u in range(2):
+                        nc.tensor.transpose(e_t[:, k, u, :], e_words[:, u * P : (u + 1) * P], identity[:])
+                nc.scalar.copy(
+                    out=e_grouped_of[g][:, 2 * pair : 2 * pair + 2, :, :].bitcast(F32),
+                    in_=e_t[:].rearrange("p k u s -> p k s u"),
+                )
+
+        def regroup_values(g):
+            b, first = divmod(g * GROUP, HEADS)
+            v_grouped_of[g] = double.tile([P, GROUP, WIDTH, PACK], BF16, name="v_grouped", align_bytes=64)
+            nc.scalar.copy(
+                out=v_grouped_of[g][:],
+                in_=v_raw_of[b][:, first : first + GROUP, :, :].rearrange("p n t i -> p n i t"),
+            )
+
+        def quantise_e(g):
+            e_codes_of[g] = double.tile([P, GROUP * P], U32, name="e_codes", align_bytes=64)
+            e_scales_of[g] = double.tile([P, GROUP * P], U8, name="e_scales", align_bytes=64)
+            nc.vector.quantize_mx(
+                out=e_codes_of[g][:].bitcast(FP8X4),
+                scales=e_scales_of[g][:],
+                in_=e_grouped_of[g][:].rearrange("p k s t -> p (k s t)"),
+            )
+
+        def quantise_values(g):
+            columns = slice(g * GROUP * WIDTH, (g + 1) * GROUP * WIDTH)
+            nc.vector.quantize_mx(
+                out=v_codes[:, columns].bitcast(FP8X4),
+                scales=v_scales[:, columns],
+                in_=v_grouped_of[g][:].rearrange("p n i t -> p (n i t)"),
+            )
+
+        def attend(g):
+            bank, first = divmod(g * GROUP, BANK_HEADS)
+            if first == 0:
+                ctx_bank_of[bank] = psum.tile([P, BANK_HEADS, WIDTH], F32, name="ctx_bank")
+            for k in range(GROUP):
+                n = g * GROUP + k
+                queries = slice(k * P, (k + 1) * P)
+                features = slice(n * WIDTH, (n + 1) * WIDTH)
+                nc.tensor.matmul_mx(
+                    out=ctx_bank_of[bank][:, first + k, :],
+                    lhsT=e_codes_of[g][:, queries].bitcast(FP8X4),
+                    lhsT_scale=e_scales_of[g][:, queries],
+                    rhs=v_codes[:, features].bitcast(FP8X4),
+                    rhs_scale=v_scales[:, features],
+                    start=True,
+                    stop=True,
+                )
+
+        def invert_rowsums(bank):
+            inverse_of[bank] = double.tile([P, BANK_HEADS], F32, name="inverse")
+            nc.vector.reciprocal(
+                out=inverse_of[bank][:], in_=rowsum[:, bank * BANK_HEADS : (bank + 1) * BANK_HEADS]
+            )
+
+        def divide(bank):
+            b, first = divmod(bank * BANK_HEADS, HEADS)
+            if first == 0:
+                c_of[b] = double.tile([P, HEADS, WIDTH], BF16, name="c")
+            nc.vector.tensor_tensor(
+                out=c_of[b][:, first : first + BANK_HEADS, :],
+                in0=ctx_bank_of[bank][:],
+                in1=inverse_of[bank][:].unsqueeze(2).to_broadcast([P, BANK_HEADS, WIDTH]),
+                op=ALU.mult,
+            )
+
+        def transpose_words(rows):
+            words = rows.bitcast(F32)
+            turned = psum.tile([P, PASSES * 2, P], F32, name="turned")
+            for block in range(PASSES * 2):
+                nc.tensor.transpose(turned[:, block, :], words[:, block * P : (block + 1) * P], identity[:])
+            return turned
+
+        def copy_words(turned, grouped):
+            nc.scalar.copy(out=grouped[:].bitcast(F32), in_=turned[:].rearrange("p (g u) r -> p g r u", u=2))
+
+        def turn_w(r):
+            w_grouped_of[r] = double.tile(
+                [P, PASSES, P, PACK], BF16, name="w_grouped", bufs=2 * W_PER_STEP, align_bytes=64
+            )
+            copy_words(transpose_words(w_raw[:, r, :]), w_grouped_of[r])
+
+        def quantise_w(r):
+            rows = slice(r * P, (r + 1) * P)
+            for g in range(PASSES):
+                nc.vector.quantize_mx(
+                    out=w_codes[:, g, rows].bitcast(FP8X4),
+                    scales=w_scales[:, g, rows],
+                    in_=w_grouped_of[r][:, g, :, :].rearrange("p r t -> p (r t)"),
+                )
+
+        def project(b):
+            c_codes = double.tile([P, PASSES * P], U32, name="c_codes", align_bytes=64)
+            c_scales = double.tile([P, PASSES * P], U8, name="c_scales", align_bytes=64)
+            nc.vector.quantize_mx(
+                out=c_codes[:].bitcast(FP8X4),
+                scales=c_scales[:],
+                in_=c_grouped_of[b][:].rearrange("p g s t -> p (g s t)"),
+            )
+            o_banks_of[b] = []
+            for half in range(FEATURES // N_TILE):
+                o_bank = psum.tile([P, N_TILE], F32, name="o_bank")
+                for g in range(PASSES):
+                    queries = slice(g * P, (g + 1) * P)
+                    outputs = slice(half * N_TILE, (half + 1) * N_TILE)
+                    nc.tensor.matmul_mx(
+                        out=o_bank[:],
+                        lhsT=c_codes[:, queries].bitcast(FP8X4),
+                        lhsT_scale=c_scales[:, queries],
+                        rhs=w_codes[:, g, outputs].bitcast(FP8X4),
+                        rhs_scale=w_scales[:, g, outputs],
+                        start=(g == 0),
+                        stop=(g == PASSES - 1),
+                    )
+                o_banks_of[b].append(o_bank)
+
+        def add_residual(b):
+            o_of[b] = double.tile([P, FEATURES], F32, name="o")
+            stats = double.tile([P, FEATURES // N_TILE, 6], F32, name="stats")
+            for half in range(FEATURES // N_TILE):
+                outputs = slice(half * N_TILE, (half + 1) * N_TILE)
+                nc.vector.tensor_tensor(
+                    out=o_of[b][:, outputs], in0=o_banks_of[b][half][:], in1=residual[:, b, outputs], op=ALU.add
+                )
+            for half in range(FEATURES // N_TILE):
+                outputs = slice(half * N_TILE, (half + 1) * N_TILE)
+                nc.vector.bn_stats(out=stats[:, half, :], in_=o_of[b][:, outputs])
+            moments_of[b] = double.tile([P, 2], F32, name="moments")
+            nc.vector.bn_aggr(out=moments_of[b][:], in_=stats[:].rearrange("p c k -> p (c k)"))
+            spread = double.tile([P, 1], F32, name="spread")
+            nc.vector.tensor_scalar_add(out=spread[:], in0=moments_of[b][:, 1:2], scalar1=LN_EPS)
+            rstd_of[b] = double.tile([P, 1], F32, name="rstd")
+            nc.gpsimd.tensor_tensor(out=rstd_of[b][:], in0=spread[:], in1=minus_half[:], op=ALU.pow)
+
+        def layer_norm(b):
+            for half in range(FEATURES // N_TILE):
+                outputs = slice(half * N_TILE, (half + 1) * N_TILE)
+                nc.vector.scalar_tensor_tensor(
+                    out=o_of[b][:, outputs], in0=o_of[b][:, outputs], scalar=moments_of[b][:, 0:1],
+                    in1=gain[:, outputs], op0=ALU.subtract, op1=ALU.mult,
+                )
+            for half in range(FEATURES // N_TILE):
+                outputs = slice(half * N_TILE, (half + 1) * N_TILE)
+                nc.vector.scalar_tensor_tensor(
+                    out=o_of[b][:, outputs], in0=o_of[b][:, outputs], scalar=rstd_of[b][:, 0:1],
+                    in1=bias[:, outputs], op0=ALU.mult, op1=ALU.add,
+                )
+                nc.gpsimd.dma_start(out=out[:, b, outputs], in_=o_of[b][:, outputs])
+
+        load_scores(0)
+        load_scores(1)
+        load_values(0)
+        load_scores(2)
+        load_scores(3)
+        nc.sync.dma_start(out=w_raw[:], in_=w_view)
+
+        hide(0)
+
+        last_step = GROUPS_PER_BATCH * (BATCH - 1) + 10
+        for step in range(last_step + 1):
+            b, phase = divmod(step - 6, GROUPS_PER_BATCH)
+            bank, odd = divmod(step - 4, BANK_GROUPS)
+            divides = odd == 0 and 0 <= bank < ALL_HEADS // BANK_HEADS
+
+            if step + 1 < GROUPS:
+                hide(step + 1)
+            if step < GROUPS:
+                add_scores(step)
+            if step + SCORE_BUFS < GROUPS:
+                load_scores(step + SCORE_BUFS)
+            if step == 1:
+                load_values(1)
+            if step == 2:
+                nc.sync.dma_start(out=residual[:], in_=inputMHA)
+                nc.sync.dma_start(out=gain[:], in_=ln_w.partition_broadcast(P))
+                nc.sync.dma_start(out=bias[:], in_=ln_b.partition_broadcast(P))
+
+            if 0 <= step - 1 < GROUPS:
+                exponentials(step - 1)
+                regroup_values(step - 1)
+                regrouped, rest = divmod(step, GROUPS_PER_BATCH)
+                if rest == 0 and regrouped + 1 < BATCH:
+                    load_values(regrouped + 1)
+            for r in range(W_ROWS):
+                if step == W_FIRST_STEP + r // W_PER_STEP:
+                    turn_w(r)
+            if phase == 1 and 0 <= b < BATCH:
+                c_grouped_of[b] = double.tile([P, PASSES, P, PACK], BF16, name="c_grouped", align_bytes=64)
+                copy_words(c_words_of[b], c_grouped_of[b])
+
+            if 0 <= step - 2 < GROUPS:
+                quantise_e(step - 2)
+            if step < GROUPS:
+                row_maxima(step)
+            if 0 <= step - 2 < GROUPS:
+                quantise_values(step - 2)
+                attend(step - 2)
+            if divides:
+                invert_rowsums(bank)
+            if step < GROUPS:
+                shifts(step)
+            for r in range(W_ROWS):
+                if step == W_FIRST_STEP + r // W_PER_STEP + 1:
+                    quantise_w(r)
+            if divides:
+                divide(bank)
+            if phase == 0 and 0 <= b < BATCH:
+                c_words_of[b] = transpose_words(c_of[b][:].rearrange("p n i -> p (n i)"))
+            if phase == 2 and 0 <= b < BATCH:
+                project(b)
+            if phase == 3 and 0 <= b < BATCH:
+                add_residual(b)
+            if phase == 0 and 0 <= b - 1 < BATCH:
+                layer_norm(b - 1)

@@ -32,7 +32,7 @@ OPEN_KEYS = KEYS - WINDOW
 HIDDEN = 1e30
 
 GROUP = 4
-POOL_HEADS = 3
+POOL_HEADS = 2
 VECTOR_HEADS = GROUP - POOL_HEADS
 GROUPS = ALL_HEADS // GROUP
 GROUPS_PER_BATCH = HEADS // GROUP
@@ -93,7 +93,7 @@ def tile_maskedmultiheadattention_pa_kernel(
         bias = const.tile([P, FEATURES], BF16)
 
         content_of, pos_of, v_raw_of = {}, {}, {}
-        sum_of, top_of, shift_of, e_grouped_of, e_codes_of, e_scales_of, v_grouped_of = {}, {}, {}, {}, {}, {}, {}
+        sum_of, top_of, shift_of, e_banks_of, e_grouped_of, e_codes_of, e_scales_of, v_grouped_of = {}, {}, {}, {}, {}, {}, {}, {}
         w_grouped_of, ctx_bank_of, inverse_of, c_of, c_words_of, c_grouped_of, o_banks_of, o_of, moments_of, rstd_of = (
             {}, {}, {}, {}, {}, {}, {}, {}, {}, {},
         )
@@ -154,16 +154,21 @@ def tile_maskedmultiheadattention_pa_kernel(
                     scale=SCALE,
                     accum_out=rowsum[:, n : n + 1],
                 )
-            e_grouped_of[g] = triple.tile([P, GROUP, P, PACK], BF16, name="e_grouped", align_bytes=64)
+            e_banks_of[g] = []
             for pair in range(GROUP // 2):
                 e_t = psum.tile([P, 2, 2, P], F32, name="e_t")
                 for k in range(2):
                     e_words = e[:, 2 * pair + k, :].bitcast(F32)
                     for u in range(2):
                         nc.tensor.transpose(e_t[:, k, u, :], e_words[:, u * P : (u + 1) * P], identity[:])
+                e_banks_of[g].append(e_t)
+
+        def copy_e(g):
+            e_grouped_of[g] = triple.tile([P, GROUP, P, PACK], BF16, name="e_grouped", align_bytes=64)
+            for pair in range(GROUP // 2):
                 nc.scalar.copy(
                     out=e_grouped_of[g][:, 2 * pair : 2 * pair + 2, :, :].bitcast(F32),
-                    in_=e_t[:].rearrange("p k u s -> p k s u"),
+                    in_=e_banks_of[g][pair][:].rearrange("p k u s -> p k s u"),
                 )
 
         def regroup_values(g):
@@ -278,19 +283,21 @@ def tile_maskedmultiheadattention_pa_kernel(
 
         def add_residual(b):
             o_of[b] = double.tile([P, FEATURES], F32, name="o")
-            stats = double.tile([P, FEATURES // N_TILE, 6], F32, name="stats")
             for half in range(FEATURES // N_TILE):
                 outputs = slice(half * N_TILE, (half + 1) * N_TILE)
                 nc.vector.tensor_tensor(
                     out=o_of[b][:, outputs], in0=o_banks_of[b][half][:], in1=residual[:, b, outputs], op=ALU.add
                 )
+
+        def moments(b):
+            stats = double.tile([P, FEATURES // N_TILE, 6], F32, name="stats")
             for half in range(FEATURES // N_TILE):
                 outputs = slice(half * N_TILE, (half + 1) * N_TILE)
                 nc.vector.bn_stats(out=stats[:, half, :], in_=o_of[b][:, outputs])
             moments_of[b] = double.tile([P, 2], F32, name="moments")
             nc.vector.bn_aggr(out=moments_of[b][:], in_=stats[:].rearrange("p c k -> p (c k)"))
             spread = double.tile([P, 1], F32, name="spread")
-            nc.vector.tensor_scalar_add(out=spread[:], in0=moments_of[b][:, 1:2], scalar1=LN_EPS)
+            nc.gpsimd.tensor_scalar_add(out=spread[:], in0=moments_of[b][:, 1:2], scalar1=LN_EPS)
             rstd_of[b] = double.tile([P, 1], F32, name="rstd")
             nc.gpsimd.tensor_tensor(out=rstd_of[b][:], in0=spread[:], in1=minus_half[:], op=ALU.pow)
 
@@ -307,7 +314,7 @@ def tile_maskedmultiheadattention_pa_kernel(
                     out=o_of[b][:, outputs], in0=o_of[b][:, outputs], scalar=rstd_of[b][:, 0:1],
                     in1=bias[:, outputs], op0=ALU.mult, op1=ALU.add,
                 )
-                nc.gpsimd.dma_start(out=out[:, b, outputs], in_=o_of[b][:, outputs])
+                nc.sync.dma_start(out=out[:, b, outputs], in_=o_of[b][:, outputs])
 
         load_scores(0)
         load_scores(1)
@@ -318,14 +325,13 @@ def tile_maskedmultiheadattention_pa_kernel(
 
         hide(0)
 
-        last_step = GROUPS_PER_BATCH * (BATCH - 1) + 10
+        last_step = GROUPS_PER_BATCH * (BATCH - 1) + 8
         for step in range(last_step + 1):
             b, phase = divmod(step - 6, GROUPS_PER_BATCH)
+            due = 0 <= b < BATCH
             bank, odd = divmod(step - 4, BANK_GROUPS)
             divides = odd == 0 and 0 <= bank < ALL_HEADS // BANK_HEADS
 
-            if step + 1 < GROUPS:
-                hide(step + 1)
             if step < GROUPS:
                 add_scores(step)
             if step + SCORE_BUFS < GROUPS:
@@ -337,40 +343,45 @@ def tile_maskedmultiheadattention_pa_kernel(
                 nc.sync.dma_start(out=gain[:], in_=ln_w.partition_broadcast(P))
                 nc.sync.dma_start(out=bias[:], in_=ln_b.partition_broadcast(P))
 
+            if due and phase == 1:
+                c_grouped_of[b] = double.tile([P, PASSES, P, PACK], BF16, name="c_grouped", align_bytes=64)
+                copy_words(c_words_of[b], c_grouped_of[b])
             if 0 <= step - 1 < GROUPS:
                 exponentials(step - 1)
                 regroup_values(step - 1)
+                copy_e(step - 1)
                 regrouped, rest = divmod(step, GROUPS_PER_BATCH)
                 if rest == 0 and regrouped + 1 < BATCH:
                     load_values(regrouped + 1)
             for r in range(W_ROWS):
                 if step == W_FIRST_STEP + r // W_PER_STEP:
                     turn_w(r)
-            if phase == 1 and 0 <= b < BATCH:
-                c_grouped_of[b] = double.tile([P, PASSES, P, PACK], BF16, name="c_grouped", align_bytes=64)
-                copy_words(c_words_of[b], c_grouped_of[b])
 
             if 0 <= step - 2 < GROUPS:
                 quantise_e(step - 2)
-            if step < GROUPS:
-                row_maxima(step)
-            if 0 <= step - 2 < GROUPS:
                 quantise_values(step - 2)
                 attend(step - 2)
-            if divides:
-                invert_rowsums(bank)
-            if step < GROUPS:
-                shifts(step)
             for r in range(W_ROWS):
                 if step == W_FIRST_STEP + r // W_PER_STEP + 1:
                     quantise_w(r)
+            if due and phase == 1:
+                project(b)
+            if divides:
+                invert_rowsums(bank)
+
+            if step + 1 < GROUPS:
+                hide(step + 1)
+            if step < GROUPS:
+                row_maxima(step)
             if divides:
                 divide(bank)
-            if phase == 0 and 0 <= b < BATCH:
+            if due and phase == 0:
                 c_words_of[b] = transpose_words(c_of[b][:].rearrange("p n i -> p (n i)"))
-            if phase == 2 and 0 <= b < BATCH:
-                project(b)
-            if phase == 3 and 0 <= b < BATCH:
+            if due and phase == 1:
                 add_residual(b)
-            if phase == 0 and 0 <= b - 1 < BATCH:
-                layer_norm(b - 1)
+            if step < GROUPS:
+                shifts(step)
+            if due and phase == 1:
+                moments(b)
+            if due and phase == 2:
+                layer_norm(b)

@@ -22,9 +22,9 @@ FEATURES = HEADS * WIDTH
 ALL_HEADS = BATCH * HEADS
 PACK = 4
 K_PASS = P * PACK
-WORDS = K_PASS // 2
 PASSES = FEATURES // K_PASS
 N_TILE = 512
+HALVES = FEATURES // N_TILE
 SCALE = 0.125
 LN_EPS = 1e-5
 WINDOW = P
@@ -37,11 +37,11 @@ VECTOR_HEADS = GROUP - POOL_HEADS
 GROUPS = ALL_HEADS // GROUP
 GROUPS_PER_BATCH = HEADS // GROUP
 BANK_HEADS = N_TILE // WIDTH
-BANK_GROUPS = BANK_HEADS // GROUP
-SCORE_BUFS = 4
+LOAD_BUFS = 4
 W_ROWS = FEATURES // P
-W_FIRST_STEP = 3
+W_FIRST_STEP = 4
 W_PER_STEP = 2
+W_LAST_STEP = W_FIRST_STEP + W_ROWS // W_PER_STEP - 1
 
 FLOPS = 2 * ALL_HEADS * P * KEYS * WIDTH + 2 * BATCH * P * FEATURES * FEATURES
 
@@ -53,7 +53,7 @@ def tile_maskedmultiheadattention_pa_kernel(
     with ExitStack() as ctx:
         ctx.enter_context(tc.manual_schedule())
         const = ctx.enter_context(tc.tile_pool(name="const", bufs=1))
-        scores_in = ctx.enter_context(tc.tile_pool(name="scores_in", bufs=SCORE_BUFS))
+        loaded = ctx.enter_context(tc.tile_pool(name="loaded", bufs=LOAD_BUFS))
         triple = ctx.enter_context(tc.tile_pool(name="triple", bufs=3))
         double = ctx.enter_context(tc.tile_pool(name="double", bufs=2))
         psum = ctx.enter_context(tc.psum_pool(name="psum", bufs=2))
@@ -92,25 +92,22 @@ def tile_maskedmultiheadattention_pa_kernel(
         gain = const.tile([P, FEATURES], BF16)
         bias = const.tile([P, FEATURES], BF16)
 
-        content_of, pos_of, v_raw_of = {}, {}, {}
-        sum_of, top_of, shift_of, e_banks_of, e_grouped_of, e_codes_of, e_scales_of, v_grouped_of = {}, {}, {}, {}, {}, {}, {}, {}
-        w_grouped_of, ctx_bank_of, inverse_of, c_of, c_words_of, c_grouped_of, o_banks_of, o_of, moments_of, rstd_of = (
-            {}, {}, {}, {}, {}, {}, {}, {}, {}, {},
-        )
+        content_of, pos_of, v_raw_of, sum_of, top_of, e_banks_of, e_grouped_of = {}, {}, {}, {}, {}, {}, {}
+        e_codes_of, e_scales_of, v_grouped_of = {}, {}, {}
+        ctx_bank_of, inverse_of, w_grouped_of = {}, {}, {}
+        c_of, c_words_of, c_grouped_of, o_banks_of, o_of, moments_of, rstd_of = {}, {}, {}, {}, {}, {}, {}
 
-        def load_scores(g):
+        def load_group(g):
             heads = slice(g * GROUP, (g + 1) * GROUP)
-            content_of[g] = scores_in.tile([P, GROUP, KEYS], BF16, name="content")
+            content_of[g] = loaded.tile([P, GROUP, KEYS], BF16, name="content")
             nc.sync.dma_start(out=content_of[g][:], in_=content_view[:, heads, :])
-            pos_of[g] = scores_in.tile([P, GROUP, KEYS], BF16, name="pos")
+            pos_of[g] = loaded.tile([P, GROUP, KEYS], BF16, name="pos")
             nc.sync.dma_start(out=pos_of[g][:, :, 0:OPEN_KEYS], in_=pos_from_0[:, heads, 0:OPEN_KEYS])
             nc.sync.dma_start(out=pos_of[g][:, :, OPEN_KEYS:KEYS], in_=pos_from_1[:, heads, OPEN_KEYS - 1 : KEYS - 1])
-
-        def load_values(b):
-            v_raw_of[b] = double.tile([P, HEADS, PACK, WIDTH], BF16, name="v_raw")
+            v_raw_of[g] = loaded.tile([P, GROUP, PACK, WIDTH], BF16, name="v_raw")
             nc.sync.dma_start(
-                out=v_raw_of[b][:].rearrange("p n (u w) i -> p (n u) (w i)", u=2),
-                in_=values_view[:, b * HEADS * 2 : (b + 1) * HEADS * 2, :],
+                out=v_raw_of[g][:].rearrange("p n (u w) i -> p (n u) (w i)", u=2),
+                in_=values_view[:, g * GROUP * 2 : (g + 1) * GROUP * 2, :],
             )
 
         def hide(g):
@@ -138,11 +135,9 @@ def tile_maskedmultiheadattention_pa_kernel(
             top_of[g] = triple.tile([P, GROUP], F32, name="top")
             nc.vector.tensor_reduce(out=top_of[g][:], in_=sum_of[g][:], axis=AXIS_X, op=ALU.max)
 
-        def shifts(g):
-            shift_of[g] = triple.tile([P, GROUP], F32, name="shift")
-            nc.vector.tensor_scalar_mul(out=shift_of[g][:], in0=top_of[g][:], scalar1=-SCALE)
-
         def exponentials(g):
+            shift = double.tile([P, GROUP], F32, name="shift")
+            nc.scalar.mul(out=shift[:], in_=top_of[g][:], mul=-SCALE)
             e = double.tile([P, GROUP, KEYS], BF16, name="e")
             for k in range(GROUP):
                 n = g * GROUP + k
@@ -150,36 +145,27 @@ def tile_maskedmultiheadattention_pa_kernel(
                     out=e[:, k, :],
                     in_=sum_of[g][:, k, :],
                     func=ACT.Exp,
-                    bias=shift_of[g][:, k : k + 1],
+                    bias=shift[:, k : k + 1],
                     scale=SCALE,
                     accum_out=rowsum[:, n : n + 1],
                 )
-            e_banks_of[g] = []
+            e_grouped_of[g] = triple.tile([P, GROUP, P, PACK], BF16, name="e_grouped", align_bytes=64)
             for pair in range(GROUP // 2):
                 e_t = psum.tile([P, 2, 2, P], F32, name="e_t")
                 for k in range(2):
                     e_words = e[:, 2 * pair + k, :].bitcast(F32)
                     for u in range(2):
                         nc.tensor.transpose(e_t[:, k, u, :], e_words[:, u * P : (u + 1) * P], identity[:])
-                e_banks_of[g].append(e_t)
-
-        def copy_e(g):
-            e_grouped_of[g] = triple.tile([P, GROUP, P, PACK], BF16, name="e_grouped", align_bytes=64)
-            for pair in range(GROUP // 2):
                 nc.scalar.copy(
                     out=e_grouped_of[g][:, 2 * pair : 2 * pair + 2, :, :].bitcast(F32),
-                    in_=e_banks_of[g][pair][:].rearrange("p k u s -> p k s u"),
+                    in_=e_t[:].rearrange("p k u s -> p k s u"),
                 )
 
         def regroup_values(g):
-            b, first = divmod(g * GROUP, HEADS)
-            v_grouped_of[g] = double.tile([P, GROUP, WIDTH, PACK], BF16, name="v_grouped", align_bytes=64)
-            nc.scalar.copy(
-                out=v_grouped_of[g][:],
-                in_=v_raw_of[b][:, first : first + GROUP, :, :].rearrange("p n t i -> p n i t"),
-            )
+            v_grouped_of[g] = triple.tile([P, GROUP, WIDTH, PACK], BF16, name="v_grouped", align_bytes=64)
+            nc.scalar.copy(out=v_grouped_of[g][:], in_=v_raw_of[g][:].rearrange("p n t i -> p n i t"))
 
-        def quantise_e(g):
+        def quantise_group(g):
             e_codes_of[g] = double.tile([P, GROUP * P], U32, name="e_codes", align_bytes=64)
             e_scales_of[g] = double.tile([P, GROUP * P], U8, name="e_scales", align_bytes=64)
             nc.vector.quantize_mx(
@@ -187,8 +173,6 @@ def tile_maskedmultiheadattention_pa_kernel(
                 scales=e_scales_of[g][:],
                 in_=e_grouped_of[g][:].rearrange("p k s t -> p (k s t)"),
             )
-
-        def quantise_values(g):
             columns = slice(g * GROUP * WIDTH, (g + 1) * GROUP * WIDTH)
             nc.vector.quantize_mx(
                 out=v_codes[:, columns].bitcast(FP8X4),
@@ -265,7 +249,7 @@ def tile_maskedmultiheadattention_pa_kernel(
                 in_=c_grouped_of[b][:].rearrange("p g s t -> p (g s t)"),
             )
             o_banks_of[b] = []
-            for half in range(FEATURES // N_TILE):
+            for half in range(HALVES):
                 o_bank = psum.tile([P, N_TILE], F32, name="o_bank")
                 for g in range(PASSES):
                     queries = slice(g * P, (g + 1) * P)
@@ -282,33 +266,31 @@ def tile_maskedmultiheadattention_pa_kernel(
                 o_banks_of[b].append(o_bank)
 
         def add_residual(b):
-            o_of[b] = double.tile([P, FEATURES], F32, name="o")
-            for half in range(FEATURES // N_TILE):
+            o_of[b] = const.tile([P, FEATURES], F32, name="o_%d" % b)
+            stats = double.tile([P, HALVES, 6], F32, name="stats")
+            for half in range(HALVES):
                 outputs = slice(half * N_TILE, (half + 1) * N_TILE)
                 nc.vector.tensor_tensor(
                     out=o_of[b][:, outputs], in0=o_banks_of[b][half][:], in1=residual[:, b, outputs], op=ALU.add
                 )
-
-        def moments(b):
-            stats = double.tile([P, FEATURES // N_TILE, 6], F32, name="stats")
-            for half in range(FEATURES // N_TILE):
+            for half in range(HALVES):
                 outputs = slice(half * N_TILE, (half + 1) * N_TILE)
                 nc.vector.bn_stats(out=stats[:, half, :], in_=o_of[b][:, outputs])
-            moments_of[b] = double.tile([P, 2], F32, name="moments")
+            moments_of[b] = const.tile([P, 2], F32, name="moments_%d" % b)
             nc.vector.bn_aggr(out=moments_of[b][:], in_=stats[:].rearrange("p c k -> p (c k)"))
             spread = double.tile([P, 1], F32, name="spread")
             nc.gpsimd.tensor_scalar_add(out=spread[:], in0=moments_of[b][:, 1:2], scalar1=LN_EPS)
-            rstd_of[b] = double.tile([P, 1], F32, name="rstd")
+            rstd_of[b] = const.tile([P, 1], F32, name="rstd_%d" % b)
             nc.gpsimd.tensor_tensor(out=rstd_of[b][:], in0=spread[:], in1=minus_half[:], op=ALU.pow)
 
         def layer_norm(b):
-            for half in range(FEATURES // N_TILE):
+            for half in range(HALVES):
                 outputs = slice(half * N_TILE, (half + 1) * N_TILE)
                 nc.vector.scalar_tensor_tensor(
                     out=o_of[b][:, outputs], in0=o_of[b][:, outputs], scalar=moments_of[b][:, 0:1],
                     in1=gain[:, outputs], op0=ALU.subtract, op1=ALU.mult,
                 )
-            for half in range(FEATURES // N_TILE):
+            for half in range(HALVES):
                 outputs = slice(half * N_TILE, (half + 1) * N_TILE)
                 nc.vector.scalar_tensor_tensor(
                     out=o_of[b][:, outputs], in0=o_of[b][:, outputs], scalar=rstd_of[b][:, 0:1],
@@ -316,58 +298,50 @@ def tile_maskedmultiheadattention_pa_kernel(
                 )
                 nc.sync.dma_start(out=out[:, b, outputs], in_=o_of[b][:, outputs])
 
-        load_scores(0)
-        load_scores(1)
-        load_values(0)
-        load_scores(2)
-        load_scores(3)
-        nc.sync.dma_start(out=w_raw[:], in_=w_view)
-
+        for g in range(LOAD_BUFS):
+            load_group(g)
         hide(0)
 
-        last_step = GROUPS_PER_BATCH * (BATCH - 1) + 8
-        for step in range(last_step + 1):
-            b, phase = divmod(step - 6, GROUPS_PER_BATCH)
-            due = 0 <= b < BATCH
-            bank, odd = divmod(step - 4, BANK_GROUPS)
-            divides = odd == 0 and 0 <= bank < ALL_HEADS // BANK_HEADS
+        def turn_step(b):
+            return max(GROUPS_PER_BATCH * (b + 1) + 1, W_LAST_STEP)
+
+        for step in range(GROUPS + BATCH):
+            bank, second = divmod(step - 2, BANK_HEADS // GROUP)
+            divides = second == 1 and 0 <= bank < ALL_HEADS // BANK_HEADS
 
             if step < GROUPS:
                 add_scores(step)
-            if step + SCORE_BUFS < GROUPS:
-                load_scores(step + SCORE_BUFS)
-            if step == 1:
-                load_values(1)
-            if step == 2:
-                nc.sync.dma_start(out=residual[:], in_=inputMHA)
-                nc.sync.dma_start(out=gain[:], in_=ln_w.partition_broadcast(P))
-                nc.sync.dma_start(out=bias[:], in_=ln_b.partition_broadcast(P))
-
-            if due and phase == 1:
-                c_grouped_of[b] = double.tile([P, PASSES, P, PACK], BF16, name="c_grouped", align_bytes=64)
-                copy_words(c_words_of[b], c_grouped_of[b])
-            if 0 <= step - 1 < GROUPS:
-                exponentials(step - 1)
-                regroup_values(step - 1)
-                copy_e(step - 1)
-                regrouped, rest = divmod(step, GROUPS_PER_BATCH)
-                if rest == 0 and regrouped + 1 < BATCH:
-                    load_values(regrouped + 1)
-            for r in range(W_ROWS):
-                if step == W_FIRST_STEP + r // W_PER_STEP:
-                    turn_w(r)
-
-            if 0 <= step - 2 < GROUPS:
-                quantise_e(step - 2)
-                quantise_values(step - 2)
-                attend(step - 2)
             for r in range(W_ROWS):
                 if step == W_FIRST_STEP + r // W_PER_STEP + 1:
                     quantise_w(r)
-            if due and phase == 1:
-                project(b)
+            for b in range(BATCH):
+                if step == turn_step(b) + 1:
+                    c_grouped_of[b] = double.tile([P, PASSES, P, PACK], BF16, name="c_grouped", align_bytes=64)
+                    copy_words(c_words_of[b], c_grouped_of[b])
+                    project(b)
+            if 0 <= step - 1 < GROUPS:
+                exponentials(step - 1)
+            if step < GROUPS:
+                regroup_values(step)
+            for r in range(W_ROWS):
+                if step == W_FIRST_STEP + r // W_PER_STEP:
+                    turn_w(r)
+            if 0 <= step - 2 < GROUPS:
+                quantise_group(step - 2)
+                attend(step - 2)
             if divides:
                 invert_rowsums(bank)
+
+            if step + LOAD_BUFS < GROUPS:
+                load_group(step + LOAD_BUFS)
+            if step < 2:
+                rows = slice(step * W_ROWS // 2, (step + 1) * W_ROWS // 2)
+                nc.sync.dma_start(out=w_raw[:, rows, :], in_=w_view[:, rows, :])
+            if step == 2:
+                nc.sync.dma_start(out=residual[:], in_=inputMHA)
+            if step == 3:
+                nc.sync.dma_start(out=gain[:], in_=ln_w.partition_broadcast(P))
+                nc.sync.dma_start(out=bias[:], in_=ln_b.partition_broadcast(P))
 
             if step + 1 < GROUPS:
                 hide(step + 1)
@@ -375,13 +349,10 @@ def tile_maskedmultiheadattention_pa_kernel(
                 row_maxima(step)
             if divides:
                 divide(bank)
-            if due and phase == 0:
-                c_words_of[b] = transpose_words(c_of[b][:].rearrange("p n i -> p (n i)"))
-            if due and phase == 1:
-                add_residual(b)
-            if step < GROUPS:
-                shifts(step)
-            if due and phase == 1:
-                moments(b)
-            if due and phase == 2:
-                layer_norm(b)
+            for b in range(BATCH):
+                if step == turn_step(b):
+                    c_words_of[b] = transpose_words(c_of[b][:].rearrange("p n i -> p (n i)"))
+                if step == turn_step(b) + 1:
+                    add_residual(b)
+            if step >= GROUPS:
+                layer_norm(step - GROUPS)

@@ -37,7 +37,7 @@ VECTOR_HEADS = GROUP - POOL_HEADS
 GROUPS = ALL_HEADS // GROUP
 GROUPS_PER_BATCH = HEADS // GROUP
 BANK_HEADS = N_TILE // WIDTH
-LOAD_BUFS = 4
+LOAD_BUFS = 5
 W_ROWS = FEATURES // P
 W_FIRST_STEP = 4
 W_PER_STEP = 2
@@ -63,7 +63,7 @@ def tile_maskedmultiheadattention_pa_kernel(
         skew = KEYS - 1
         pos_from_0 = pos_flat[:, P - 1 : P - 1 + P * skew].rearrange("n (s j) -> s n j", j=skew)
         pos_from_1 = pos_flat[:, P : P + P * skew].rearrange("n (s j) -> s n j", j=skew)
-        values_view = values.rearrange("b h (u p w) i -> p (b h u) (w i)", u=2, p=P, w=2)
+        values_view = values.rearrange("b h (p t) i -> p (b h) (t i)", t=PACK)
         w_view = W_out.rearrange("(r p) f -> p r f", p=P)
 
         identity = const.tile([P, P], F32)
@@ -99,16 +99,13 @@ def tile_maskedmultiheadattention_pa_kernel(
 
         def load_group(g):
             heads = slice(g * GROUP, (g + 1) * GROUP)
+            pos_of[g] = loaded.tile([P, GROUP, KEYS], BF16, name="pos")
+            nc.sync.dma_start(out=pos_of[g][:, :, OPEN_KEYS:KEYS], in_=pos_from_1[:, heads, OPEN_KEYS - 1 : KEYS - 1])
+            nc.sync.dma_start(out=pos_of[g][:, :, 0:OPEN_KEYS], in_=pos_from_0[:, heads, 0:OPEN_KEYS])
             content_of[g] = loaded.tile([P, GROUP, KEYS], BF16, name="content")
             nc.sync.dma_start(out=content_of[g][:], in_=content_view[:, heads, :])
-            pos_of[g] = loaded.tile([P, GROUP, KEYS], BF16, name="pos")
-            nc.sync.dma_start(out=pos_of[g][:, :, 0:OPEN_KEYS], in_=pos_from_0[:, heads, 0:OPEN_KEYS])
-            nc.sync.dma_start(out=pos_of[g][:, :, OPEN_KEYS:KEYS], in_=pos_from_1[:, heads, OPEN_KEYS - 1 : KEYS - 1])
             v_raw_of[g] = loaded.tile([P, GROUP, PACK, WIDTH], BF16, name="v_raw")
-            nc.sync.dma_start(
-                out=v_raw_of[g][:].rearrange("p n (u w) i -> p (n u) (w i)", u=2),
-                in_=values_view[:, g * GROUP * 2 : (g + 1) * GROUP * 2, :],
-            )
+            nc.sync.dma_start(out=v_raw_of[g][:].rearrange("p n t i -> p n (t i)"), in_=values_view[:, heads, :])
 
         def hide(g):
             window = pos_of[g][:, :, OPEN_KEYS:KEYS]
@@ -155,7 +152,7 @@ def tile_maskedmultiheadattention_pa_kernel(
                 for k in range(2):
                     e_words = e[:, 2 * pair + k, :].bitcast(F32)
                     for u in range(2):
-                        nc.tensor.transpose(e_t[:, k, u, :], e_words[:, u * P : (u + 1) * P], identity[:])
+                        nc.tensor.transpose(e_t[:, k, u, :], e_words[:, u : 2 * P : 2], identity[:])
                 nc.scalar.copy(
                     out=e_grouped_of[g][:, 2 * pair : 2 * pair + 2, :, :].bitcast(F32),
                     in_=e_t[:].rearrange("p k u s -> p k s u"),
@@ -218,8 +215,11 @@ def tile_maskedmultiheadattention_pa_kernel(
         def transpose_words(rows):
             words = rows.bitcast(F32)
             turned = psum.tile([P, PASSES * 2, P], F32, name="turned")
-            for block in range(PASSES * 2):
-                nc.tensor.transpose(turned[:, block, :], words[:, block * P : (block + 1) * P], identity[:])
+            for g in range(PASSES):
+                for u in range(2):
+                    nc.tensor.transpose(
+                        turned[:, 2 * g + u, :], words[:, 2 * P * g + u : 2 * P * (g + 1) : 2], identity[:]
+                    )
             return turned
 
         def copy_words(turned, grouped):
@@ -339,7 +339,7 @@ def tile_maskedmultiheadattention_pa_kernel(
                 nc.sync.dma_start(out=w_raw[:, rows, :], in_=w_view[:, rows, :])
             if step == 2:
                 nc.sync.dma_start(out=residual[:], in_=inputMHA)
-            if step == 3:
+            if step == GROUPS - LOAD_BUFS:
                 nc.sync.dma_start(out=gain[:], in_=ln_w.partition_broadcast(P))
                 nc.sync.dma_start(out=bias[:], in_=ln_b.partition_broadcast(P))
 

@@ -32,8 +32,6 @@ OPEN_KEYS = KEYS - WINDOW
 HIDDEN = 1e30
 
 GROUP = 4
-POOL_HEADS = 2
-VECTOR_HEADS = GROUP - POOL_HEADS
 GROUPS = ALL_HEADS // GROUP
 GROUPS_PER_BATCH = HEADS // GROUP
 BANK_HEADS = N_TILE // WIDTH
@@ -97,6 +95,9 @@ def tile_maskedmultiheadattention_pa_kernel(
         ctx_bank_of, inverse_of, w_grouped_of = {}, {}, {}
         c_of, c_words_of, c_grouped_of, o_banks_of, o_of, moments_of, rstd_of = {}, {}, {}, {}, {}, {}, {}
 
+        def vector_heads(g):
+            return 2 if g % 2 == 0 else 3
+
         def load_group(g):
             heads = slice(g * GROUP, (g + 1) * GROUP)
             pos_of[g] = loaded.tile([P, GROUP, KEYS], BF16, name="pos")
@@ -113,19 +114,15 @@ def tile_maskedmultiheadattention_pa_kernel(
                 out=window, in0=window, in1=cap[:].unsqueeze(1).to_broadcast([P, GROUP, WINDOW]), op=ALU.min
             )
             sum_of[g] = triple.tile([P, GROUP, KEYS], F32, name="score_sum")
+            heads = slice(vector_heads(g), GROUP)
             nc.gpsimd.tensor_tensor(
-                out=sum_of[g][:, VECTOR_HEADS:GROUP, :],
-                in0=content_of[g][:, VECTOR_HEADS:GROUP, :],
-                in1=pos_of[g][:, VECTOR_HEADS:GROUP, :],
-                op=ALU.add,
+                out=sum_of[g][:, heads, :], in0=content_of[g][:, heads, :], in1=pos_of[g][:, heads, :], op=ALU.add
             )
 
         def add_scores(g):
+            heads = slice(0, vector_heads(g))
             nc.vector.tensor_tensor(
-                out=sum_of[g][:, 0:VECTOR_HEADS, :],
-                in0=content_of[g][:, 0:VECTOR_HEADS, :],
-                in1=pos_of[g][:, 0:VECTOR_HEADS, :],
-                op=ALU.add,
+                out=sum_of[g][:, heads, :], in0=content_of[g][:, heads, :], in1=pos_of[g][:, heads, :], op=ALU.add
             )
 
         def row_maxima(g):

@@ -35,6 +35,7 @@ GROUP = 4
 GROUPS = ALL_HEADS // GROUP
 GROUPS_PER_BATCH = HEADS // GROUP
 BANK_HEADS = N_TILE // WIDTH
+RUN = 4
 LOAD_BUFS = 5
 W_ROWS = FEATURES // P
 W_FIRST_STEP = 4
@@ -157,7 +158,11 @@ def tile_maskedmultiheadattention_pa_kernel(
 
         def regroup_values(g):
             v_grouped_of[g] = triple.tile([P, GROUP, WIDTH, PACK], BF16, name="v_grouped", align_bytes=64)
-            nc.scalar.copy(out=v_grouped_of[g][:], in_=v_raw_of[g][:].rearrange("p n t i -> p n i t"))
+            for k in range(GROUP):
+                nc.scalar.copy(
+                    out=v_grouped_of[g][:, k, :, :].rearrange("p (c i) t -> p c t i", i=RUN),
+                    in_=v_raw_of[g][:, k, :, :].rearrange("p t (c i) -> p c t i", i=RUN),
+                )
 
         def quantise_group(g):
             e_codes_of[g] = double.tile([P, GROUP * P], U32, name="e_codes", align_bytes=64)

@@ -31,16 +31,20 @@ WINDOW = P
 OPEN_KEYS = KEYS - WINDOW
 HIDDEN = 1e30
 
-GROUP = 4
-GROUPS = ALL_HEADS // GROUP
-GROUPS_PER_BATCH = HEADS // GROUP
+GROUP_SIZES = (1, 1, 2) + 14 * (4,) + (2, 2)
+GROUPS = len(GROUP_SIZES)
+FIRST_HEAD = [sum(GROUP_SIZES[:g]) for g in range(GROUPS)]
+MAX_GROUP = 4
 BANK_HEADS = N_TILE // WIDTH
+BANKS = ALL_HEADS // BANK_HEADS
+LAST_GROUP = [max(g for g in range(GROUPS) if FIRST_HEAD[g] < (q + 1) * BANK_HEADS) for q in range(BANKS)]
+LOAD_BUFS = 6
+SUMMED_BY_TENSOR = (GROUPS - 2, GROUPS - 1)
 RUN = 4
-LOAD_BUFS = 5
 W_ROWS = FEATURES // P
-W_FIRST_STEP = 4
+W_FIRST_STEP = 6
 W_PER_STEP = 2
-W_LAST_STEP = W_FIRST_STEP + W_ROWS // W_PER_STEP - 1
+W_READY = W_FIRST_STEP + W_ROWS // W_PER_STEP
 
 FLOPS = 2 * ALL_HEADS * P * KEYS * WIDTH + 2 * BATCH * P * FEATURES * FEATURES
 
@@ -65,23 +69,32 @@ def tile_maskedmultiheadattention_pa_kernel(
         values_view = values.rearrange("b h (p t) i -> p (b h) (t i)", t=PACK)
         w_view = W_out.rearrange("(r p) f -> p r f", p=P)
 
-        identity = const.tile([P, P], F32)
-        make_identity(nc, identity[:])
-        minus_half = const.tile([P, 1], F32)
-        nc.vector.memset(minus_half[:], -0.5)
-        table_warmer = const.tile([P, 1], F32)
-        nc.scalar.activation(out=table_warmer[:], in_=minus_half[:], func=ACT.Exp)
-
         mask_words = const.tile([P, WINDOW, 2], I32)
         nc.sync.dma_start(
             out=mask_words[:].rearrange("p j w -> p (j w)"), in_=mask.bitcast(I32)[:, 2 * OPEN_KEYS : 2 * KEYS]
         )
+        identity = const.tile([P, P], F32)
+        make_identity(nc, identity[:])
+        identity_bf16 = const.tile([P, P], BF16)
+        make_identity(nc, identity_bf16[:])
+        minus_half = const.tile([P, 1], F32)
+        nc.vector.memset(minus_half[:], -0.5)
+        table_warmer = const.tile([P, 1], F32)
+        nc.scalar.activation(out=table_warmer[:], in_=minus_half[:], func=ACT.Exp)
         cap = const.tile([P, WINDOW], BF16)
         nc.vector.tensor_scalar(
             out=cap[:], in0=mask_words[:, :, 0], scalar1=-2.0 * HIDDEN, scalar2=HIDDEN, op0=ALU.mult, op1=ALU.add
         )
 
+        hidden = const.tile([P, WINDOW], BF16)
+
+        def make_hidden():
+            nc.vector.tensor_scalar(
+                out=hidden[:], in0=mask_words[:, :, 0], scalar1=-HIDDEN, scalar2=0.0, op0=ALU.mult, op1=ALU.add
+            )
+
         rowsum = const.tile([P, ALL_HEADS], F32)
+        inverse = const.tile([P, ALL_HEADS], F32)
         v_codes = const.tile([P, ALL_HEADS * WIDTH], U32, align_bytes=64)
         v_scales = const.tile([P, ALL_HEADS * WIDTH], U8, align_bytes=64)
         w_raw = const.tile([P, W_ROWS, FEATURES], BF16)
@@ -91,88 +104,144 @@ def tile_maskedmultiheadattention_pa_kernel(
         gain = const.tile([P, FEATURES], BF16)
         bias = const.tile([P, FEATURES], BF16)
 
-        content_of, pos_of, v_raw_of, sum_of, top_of, e_banks_of, e_grouped_of = {}, {}, {}, {}, {}, {}, {}
-        e_codes_of, e_scales_of, v_grouped_of = {}, {}, {}
-        ctx_bank_of, inverse_of, w_grouped_of = {}, {}, {}
-        c_of, c_words_of, c_grouped_of, o_banks_of, o_of, moments_of, rstd_of = {}, {}, {}, {}, {}, {}, {}
+        head_sums_of = {}
+        content_of, pos_of, v_raw_of, sum_of, top_of, e_grouped_of = {}, {}, {}, {}, {}, {}
+        e_codes_of, e_scales_of, v_grouped_of, ctx_bank_of = {}, {}, {}, {}
+        w_grouped_of, c_of, c_words_of, c_grouped_of, c_codes_of, c_scales_of = {}, {}, {}, {}, {}, {}
+        o_banks_of, o_of, mean_of, rstd_of, sums_of, square_sum_of = {}, {}, {}, {}, {}, {}
 
-        def vector_heads(g):
-            return 2 if g % 2 == 0 else 3
+        def heads_of(g):
+            return range(FIRST_HEAD[g], FIRST_HEAD[g] + GROUP_SIZES[g])
 
-        def load_group(g):
-            heads = slice(g * GROUP, (g + 1) * GROUP)
-            pos_of[g] = loaded.tile([P, GROUP, KEYS], BF16, name="pos")
+        def vector_columns(g):
+            if GROUP_SIZES[g] == 1:
+                return KEYS
+            if GROUP_SIZES[g] == 2:
+                return KEYS
+            return 2 * KEYS if (g - 3) in LAST_GROUP else 5 * KEYS // 2
+
+        def load_scores(g):
+            n, size = FIRST_HEAD[g], GROUP_SIZES[g]
+            heads = slice(n, n + size)
+            pos_of[g] = loaded.tile([P, size, KEYS], BF16, name="pos")
             nc.sync.dma_start(out=pos_of[g][:, :, OPEN_KEYS:KEYS], in_=pos_from_1[:, heads, OPEN_KEYS - 1 : KEYS - 1])
             nc.sync.dma_start(out=pos_of[g][:, :, 0:OPEN_KEYS], in_=pos_from_0[:, heads, 0:OPEN_KEYS])
-            content_of[g] = loaded.tile([P, GROUP, KEYS], BF16, name="content")
+            content_of[g] = loaded.tile([P, size, KEYS], BF16, name="content")
             nc.sync.dma_start(out=content_of[g][:], in_=content_view[:, heads, :])
-            v_raw_of[g] = loaded.tile([P, GROUP, PACK, WIDTH], BF16, name="v_raw")
-            nc.sync.dma_start(out=v_raw_of[g][:].rearrange("p n t i -> p n (t i)"), in_=values_view[:, heads, :])
+
+        def load_values(g):
+            n, size = FIRST_HEAD[g], GROUP_SIZES[g]
+            v_raw_of[g] = loaded.tile([P, size, PACK, WIDTH], BF16, name="v_raw")
+            nc.sync.dma_start(
+                out=v_raw_of[g][:].rearrange("p n t i -> p n (t i)"), in_=values_view[:, n : n + size, :]
+            )
+
+        def flat(tile):
+            return tile[:].rearrange("p n j -> p (n j)")
 
         def hide(g):
+            if g in SUMMED_BY_TENSOR:
+                return
+            size = GROUP_SIZES[g]
             window = pos_of[g][:, :, OPEN_KEYS:KEYS]
             nc.vector.tensor_tensor(
-                out=window, in0=window, in1=cap[:].unsqueeze(1).to_broadcast([P, GROUP, WINDOW]), op=ALU.min
+                out=window, in0=window, in1=cap[:].unsqueeze(1).to_broadcast([P, size, WINDOW]), op=ALU.min
             )
-            sum_of[g] = triple.tile([P, GROUP, KEYS], F32, name="score_sum")
-            heads = slice(vector_heads(g), GROUP)
-            nc.gpsimd.tensor_tensor(
-                out=sum_of[g][:, heads, :], in0=content_of[g][:, heads, :], in1=pos_of[g][:, heads, :], op=ALU.add
-            )
+            sum_of[g] = triple.tile([P, size, KEYS], F32, name="score_sum")
+            head_sums_of[g] = [sum_of[g][:, k, :] for k in range(size)]
+            first = vector_columns(g)
+            if first < size * KEYS:
+                columns = slice(first, size * KEYS)
+                nc.gpsimd.tensor_tensor(
+                    out=flat(sum_of[g])[:, columns],
+                    in0=flat(content_of[g])[:, columns],
+                    in1=flat(pos_of[g])[:, columns],
+                    op=ALU.add,
+                )
 
         def add_scores(g):
-            heads = slice(0, vector_heads(g))
+            if g in SUMMED_BY_TENSOR:
+                return
+            columns = slice(0, vector_columns(g))
             nc.vector.tensor_tensor(
-                out=sum_of[g][:, heads, :], in0=content_of[g][:, heads, :], in1=pos_of[g][:, heads, :], op=ALU.add
+                out=flat(sum_of[g])[:, columns],
+                in0=flat(content_of[g])[:, columns],
+                in1=flat(pos_of[g])[:, columns],
+                op=ALU.add,
             )
 
+        def sum_by_tensor(g):
+            head_sums_of[g] = []
+            for k in range(GROUP_SIZES[g]):
+                if g == GROUPS - 1:
+                    head_sum = psum.tile([P, KEYS], F32, name="o_bank")
+                else:
+                    head_sum = psum.tile([P, KEYS], F32, name="turned")
+                nc.tensor.matmul(
+                    head_sum[:], lhsT=identity_bf16[:], rhs=content_of[g][:, k, :], start=True, stop=False
+                )
+                nc.tensor.matmul(
+                    head_sum[:, OPEN_KEYS:KEYS], lhsT=identity_bf16[:], rhs=hidden[:], start=False, stop=False
+                )
+                nc.tensor.matmul(head_sum[:], lhsT=identity_bf16[:], rhs=pos_of[g][:, k, :], start=False, stop=True)
+                head_sums_of[g].append(head_sum[:])
+
         def row_maxima(g):
-            top_of[g] = triple.tile([P, GROUP], F32, name="top")
+            top_of[g] = triple.tile([P, GROUP_SIZES[g]], F32, name="top")
+            if g in SUMMED_BY_TENSOR:
+                for k in range(GROUP_SIZES[g]):
+                    nc.vector.tensor_reduce(
+                        out=top_of[g][:, k : k + 1], in_=head_sums_of[g][k], axis=AXIS_X, op=ALU.max
+                    )
+                return
             nc.vector.tensor_reduce(out=top_of[g][:], in_=sum_of[g][:], axis=AXIS_X, op=ALU.max)
 
         def exponentials(g):
-            shift = double.tile([P, GROUP], F32, name="shift")
+            size = GROUP_SIZES[g]
+            shift = double.tile([P, size], F32, name="shift")
             nc.scalar.mul(out=shift[:], in_=top_of[g][:], mul=-SCALE)
-            e = double.tile([P, GROUP, KEYS], BF16, name="e")
-            for k in range(GROUP):
-                n = g * GROUP + k
+            e = double.tile([P, size, KEYS], BF16, name="e")
+            for k, n in enumerate(heads_of(g)):
                 nc.scalar.activation(
                     out=e[:, k, :],
-                    in_=sum_of[g][:, k, :],
+                    in_=head_sums_of[g][k],
                     func=ACT.Exp,
                     bias=shift[:, k : k + 1],
                     scale=SCALE,
                     accum_out=rowsum[:, n : n + 1],
                 )
-            e_grouped_of[g] = triple.tile([P, GROUP, P, PACK], BF16, name="e_grouped", align_bytes=64)
-            for pair in range(GROUP // 2):
-                e_t = psum.tile([P, 2, 2, P], F32, name="e_t")
-                for k in range(2):
-                    e_words = e[:, 2 * pair + k, :].bitcast(F32)
+            e_grouped_of[g] = triple.tile([P, size, P, PACK], BF16, name="e_grouped", align_bytes=64)
+            for first in range(0, size, 2):
+                pair = range(first, min(first + 2, size))
+                e_t = psum.tile([P, len(pair), 2, P], F32, name="e_t")
+                for k in pair:
+                    e_words = e[:, k, :].bitcast(F32)
                     for u in range(2):
-                        nc.tensor.transpose(e_t[:, k, u, :], e_words[:, u : 2 * P : 2], identity[:])
+                        nc.tensor.transpose(e_t[:, k - first, u, :], e_words[:, u : 2 * P : 2], identity[:])
                 nc.scalar.copy(
-                    out=e_grouped_of[g][:, 2 * pair : 2 * pair + 2, :, :].bitcast(F32),
+                    out=e_grouped_of[g][:, first : first + len(pair), :, :].bitcast(F32),
                     in_=e_t[:].rearrange("p k u s -> p k s u"),
                 )
 
         def regroup_values(g):
-            v_grouped_of[g] = triple.tile([P, GROUP, WIDTH, PACK], BF16, name="v_grouped", align_bytes=64)
-            for k in range(GROUP):
+            size = GROUP_SIZES[g]
+            v_grouped_of[g] = triple.tile([P, size, WIDTH, PACK], BF16, name="v_grouped", align_bytes=64)
+            for k in range(size):
                 nc.scalar.copy(
                     out=v_grouped_of[g][:, k, :, :].rearrange("p (c i) t -> p c t i", i=RUN),
                     in_=v_raw_of[g][:, k, :, :].rearrange("p t (c i) -> p c t i", i=RUN),
                 )
 
         def quantise_group(g):
-            e_codes_of[g] = double.tile([P, GROUP * P], U32, name="e_codes", align_bytes=64)
-            e_scales_of[g] = double.tile([P, GROUP * P], U8, name="e_scales", align_bytes=64)
+            size = GROUP_SIZES[g]
+            e_codes_of[g] = double.tile([P, size * P], U32, name="e_codes", align_bytes=64)
+            e_scales_of[g] = double.tile([P, size * P], U8, name="e_scales", align_bytes=64)
             nc.vector.quantize_mx(
                 out=e_codes_of[g][:].bitcast(FP8X4),
                 scales=e_scales_of[g][:],
                 in_=e_grouped_of[g][:].rearrange("p k s t -> p (k s t)"),
             )
-            columns = slice(g * GROUP * WIDTH, (g + 1) * GROUP * WIDTH)
+            columns = slice(FIRST_HEAD[g] * WIDTH, (FIRST_HEAD[g] + size) * WIDTH)
             nc.vector.quantize_mx(
                 out=v_codes[:, columns].bitcast(FP8X4),
                 scales=v_scales[:, columns],
@@ -180,15 +249,14 @@ def tile_maskedmultiheadattention_pa_kernel(
             )
 
         def attend(g):
-            bank, first = divmod(g * GROUP, BANK_HEADS)
-            if first == 0:
-                ctx_bank_of[bank] = psum.tile([P, BANK_HEADS, WIDTH], F32, name="ctx_bank")
-            for k in range(GROUP):
-                n = g * GROUP + k
+            for k, n in enumerate(heads_of(g)):
+                bank, place = divmod(n, BANK_HEADS)
+                if place == 0:
+                    ctx_bank_of[bank] = psum.tile([P, BANK_HEADS, WIDTH], F32, name="ctx_bank")
                 queries = slice(k * P, (k + 1) * P)
                 features = slice(n * WIDTH, (n + 1) * WIDTH)
                 nc.tensor.matmul_mx(
-                    out=ctx_bank_of[bank][:, first + k, :],
+                    out=ctx_bank_of[bank][:, place, :],
                     lhsT=e_codes_of[g][:, queries].bitcast(FP8X4),
                     lhsT_scale=e_scales_of[g][:, queries],
                     rhs=v_codes[:, features].bitcast(FP8X4),
@@ -197,27 +265,38 @@ def tile_maskedmultiheadattention_pa_kernel(
                     stop=True,
                 )
 
-        def invert_rowsums(bank):
-            inverse_of[bank] = double.tile([P, BANK_HEADS], F32, name="inverse")
-            nc.vector.reciprocal(
-                out=inverse_of[bank][:], in_=rowsum[:, bank * BANK_HEADS : (bank + 1) * BANK_HEADS]
-            )
+        def divided_heads(g):
+            end = FIRST_HEAD[g] + GROUP_SIZES[g]
+            if g == GROUPS - 1:
+                return FIRST_HEAD[g], end
+            if g == GROUPS - 2:
+                return FIRST_HEAD[LAST_GROUP[BANKS - 2] + 1], end
+            if g in LAST_GROUP:
+                return end - BANK_HEADS, end
+            return end, end
 
-        def divide(bank):
-            b, first = divmod(bank * BANK_HEADS, HEADS)
+        def invert_rowsums(start, end):
+            if start < end:
+                nc.vector.reciprocal(out=inverse[:, start:end], in_=rowsum[:, start:end])
+
+        def divide(start, end):
+            if start == end:
+                return
+            bank, first = divmod(start, BANK_HEADS)
+            size = end - start
             if first == 0:
-                c_of[b] = double.tile([P, HEADS, WIDTH], BF16, name="c")
+                c_of[bank] = double.tile([P, BANK_HEADS, WIDTH], BF16, name="c")
             nc.vector.tensor_tensor(
-                out=c_of[b][:, first : first + BANK_HEADS, :],
-                in0=ctx_bank_of[bank][:],
-                in1=inverse_of[bank][:].unsqueeze(2).to_broadcast([P, BANK_HEADS, WIDTH]),
+                out=c_of[bank][:, first : first + size, :],
+                in0=ctx_bank_of[bank][:, first : first + size, :],
+                in1=inverse[:, start:end].unsqueeze(2).to_broadcast([P, size, WIDTH]),
                 op=ALU.mult,
             )
 
-        def transpose_words(rows):
+        def transpose_words(rows, passes):
             words = rows.bitcast(F32)
-            turned = psum.tile([P, PASSES * 2, P], F32, name="turned")
-            for g in range(PASSES):
+            turned = psum.tile([P, passes * 2, P], F32, name="turned")
+            for g in range(passes):
                 for u in range(2):
                     nc.tensor.transpose(
                         turned[:, 2 * g + u, :], words[:, 2 * P * g + u : 2 * P * (g + 1) : 2], identity[:]
@@ -231,7 +310,7 @@ def tile_maskedmultiheadattention_pa_kernel(
             w_grouped_of[r] = double.tile(
                 [P, PASSES, P, PACK], BF16, name="w_grouped", bufs=2 * W_PER_STEP, align_bytes=64
             )
-            copy_words(transpose_words(w_raw[:, r, :]), w_grouped_of[r])
+            copy_words(transpose_words(w_raw[:, r, :], PASSES), w_grouped_of[r])
 
         def quantise_w(r):
             rows = slice(r * P, (r + 1) * P)
@@ -242,33 +321,49 @@ def tile_maskedmultiheadattention_pa_kernel(
                     in_=w_grouped_of[r][:, g, :, :].rearrange("p r t -> p (r t)"),
                 )
 
-        def project(b):
-            c_codes = double.tile([P, PASSES * P], U32, name="c_codes", align_bytes=64)
-            c_scales = double.tile([P, PASSES * P], U8, name="c_scales", align_bytes=64)
+        def turn_c(q):
+            c_words_of[q] = transpose_words(c_of[q][:].rearrange("p n i -> p (n i)"), 1)
+
+        def copy_c(q):
+            c_grouped_of[q] = double.tile([P, 1, P, PACK], BF16, name="c_grouped", align_bytes=64)
+            copy_words(c_words_of[q], c_grouped_of[q])
+
+        def quantise_c(q):
+            c_codes_of[q] = double.tile([P, P], U32, name="c_codes", bufs=4, align_bytes=64)
+            c_scales_of[q] = double.tile([P, P], U8, name="c_scales", bufs=4, align_bytes=64)
             nc.vector.quantize_mx(
-                out=c_codes[:].bitcast(FP8X4),
-                scales=c_scales[:],
-                in_=c_grouped_of[b][:].rearrange("p g s t -> p (g s t)"),
+                out=c_codes_of[q][:].bitcast(FP8X4),
+                scales=c_scales_of[q][:],
+                in_=c_grouped_of[q][:].rearrange("p g s t -> p (g s t)"),
             )
-            o_banks_of[b] = []
+
+        def project(q):
+            b, g = divmod(q, PASSES)
+            if g == 0:
+                o_banks_of[b] = [psum.tile([P, N_TILE], F32, name="o_bank") for half in range(HALVES)]
             for half in range(HALVES):
-                o_bank = psum.tile([P, N_TILE], F32, name="o_bank")
-                for g in range(PASSES):
-                    queries = slice(g * P, (g + 1) * P)
-                    outputs = slice(half * N_TILE, (half + 1) * N_TILE)
-                    nc.tensor.matmul_mx(
-                        out=o_bank[:],
-                        lhsT=c_codes[:, queries].bitcast(FP8X4),
-                        lhsT_scale=c_scales[:, queries],
-                        rhs=w_codes[:, g, outputs].bitcast(FP8X4),
-                        rhs_scale=w_scales[:, g, outputs],
-                        start=(g == 0),
-                        stop=(g == PASSES - 1),
-                    )
-                o_banks_of[b].append(o_bank)
+                outputs = slice(half * N_TILE, (half + 1) * N_TILE)
+                nc.tensor.matmul_mx(
+                    out=o_banks_of[b][half][:],
+                    lhsT=c_codes_of[q][:].bitcast(FP8X4),
+                    lhsT_scale=c_scales_of[q][:],
+                    rhs=w_codes[:, g, outputs].bitcast(FP8X4),
+                    rhs_scale=w_scales[:, g, outputs],
+                    start=(g == 0),
+                    stop=(g == PASSES - 1),
+                )
 
         def add_residual(b):
             o_of[b] = const.tile([P, FEATURES], F32, name="o_%d" % b)
+            if b < BATCH - 1:
+                sums_of[b] = const.tile([P, HALVES], F32, name="sums_%d" % b)
+                for half in range(HALVES):
+                    outputs = slice(half * N_TILE, (half + 1) * N_TILE)
+                    nc.vector.scalar_tensor_tensor(
+                        out=o_of[b][:, outputs], in0=o_banks_of[b][half][:], scalar=1.0, in1=residual[:, b, outputs],
+                        op0=ALU.mult, op1=ALU.add, accum_out=sums_of[b][:, half : half + 1],
+                    )
+                return
             stats = double.tile([P, HALVES, 6], F32, name="stats")
             for half in range(HALVES):
                 outputs = slice(half * N_TILE, (half + 1) * N_TILE)
@@ -278,21 +373,48 @@ def tile_maskedmultiheadattention_pa_kernel(
             for half in range(HALVES):
                 outputs = slice(half * N_TILE, (half + 1) * N_TILE)
                 nc.vector.bn_stats(out=stats[:, half, :], in_=o_of[b][:, outputs])
-            moments_of[b] = const.tile([P, 2], F32, name="moments_%d" % b)
-            nc.vector.bn_aggr(out=moments_of[b][:], in_=stats[:].rearrange("p c k -> p (c k)"))
+            moments = const.tile([P, 2], F32, name="moments")
+            nc.vector.bn_aggr(out=moments[:], in_=stats[:].rearrange("p c k -> p (c k)"))
+            mean_of[b] = moments[:, 0:1]
             spread = double.tile([P, 1], F32, name="spread")
-            nc.gpsimd.tensor_scalar_add(out=spread[:], in0=moments_of[b][:, 1:2], scalar1=LN_EPS)
+            nc.gpsimd.tensor_scalar_add(out=spread[:], in0=moments[:, 1:2], scalar1=LN_EPS)
             rstd_of[b] = const.tile([P, 1], F32, name="rstd_%d" % b)
             nc.gpsimd.tensor_tensor(out=rstd_of[b][:], in0=spread[:], in1=minus_half[:], op=ALU.pow)
 
-        def layer_norm(b):
-            for half in range(HALVES):
+        def find_mean(b):
+            total = double.tile([P, 1], F32, name="total")
+            nc.gpsimd.tensor_tensor(out=total[:], in0=sums_of[b][:, 0:1], in1=sums_of[b][:, 1:2], op=ALU.add)
+            mean = const.tile([P, 1], F32, name="mean_%d" % b)
+            nc.gpsimd.tensor_scalar(
+                out=mean[:], in0=total[:], scalar1=1.0 / FEATURES, scalar2=0.0, op0=ALU.mult, op1=ALU.add
+            )
+            mean_of[b] = mean[:]
+
+        def square(b):
+            squares = double.tile([P, FEATURES], BF16, name="squares")
+            square_sum_of[b] = const.tile([P, 1], F32, name="square_sum_%d" % b)
+            nc.scalar.activation(out=squares[:], in_=o_of[b][:], func=ACT.Square, accum_out=square_sum_of[b][:])
+
+        def find_rstd(b):
+            work = double.tile([P, 3], F32, name="work")
+            nc.gpsimd.tensor_tensor(out=work[:, 0:1], in0=mean_of[b], in1=mean_of[b], op=ALU.mult)
+            nc.gpsimd.tensor_scalar(
+                out=work[:, 1:2], in0=square_sum_of[b][:], scalar1=1.0 / FEATURES, scalar2=LN_EPS,
+                op0=ALU.mult, op1=ALU.add,
+            )
+            nc.gpsimd.tensor_tensor(out=work[:, 2:3], in0=work[:, 1:2], in1=work[:, 0:1], op=ALU.subtract)
+            rstd_of[b] = const.tile([P, 1], F32, name="rstd_%d" % b)
+            nc.gpsimd.tensor_tensor(out=rstd_of[b][:], in0=work[:, 2:3], in1=minus_half[:], op=ALU.pow)
+
+        def layer_norm_parts(b):
+            def centre(half):
                 outputs = slice(half * N_TILE, (half + 1) * N_TILE)
                 nc.vector.scalar_tensor_tensor(
-                    out=o_of[b][:, outputs], in0=o_of[b][:, outputs], scalar=moments_of[b][:, 0:1],
+                    out=o_of[b][:, outputs], in0=o_of[b][:, outputs], scalar=mean_of[b],
                     in1=gain[:, outputs], op0=ALU.subtract, op1=ALU.mult,
                 )
-            for half in range(HALVES):
+
+            def finish(half):
                 outputs = slice(half * N_TILE, (half + 1) * N_TILE)
                 nc.vector.scalar_tensor_tensor(
                     out=o_of[b][:, outputs], in0=o_of[b][:, outputs], scalar=rstd_of[b][:, 0:1],
@@ -300,42 +422,79 @@ def tile_maskedmultiheadattention_pa_kernel(
                 )
                 nc.sync.dma_start(out=out[:, b, outputs], in_=o_of[b][:, outputs])
 
-        for g in range(LOAD_BUFS):
-            load_group(g)
+            return [lambda: centre(0), lambda: centre(1), lambda: finish(0), lambda: finish(1)]
+
+        for g in range(3):
+            load_scores(g)
+        for g in range(3):
+            load_values(g)
+        for g in range(3, LOAD_BUFS):
+            load_scores(g)
+            load_values(g)
         hide(0)
 
-        def turn_step(b):
-            return max(GROUPS_PER_BATCH * (b + 1) + 1, W_LAST_STEP)
+        def project_step(q):
+            b, g = divmod(q, PASSES)
+            return max(LAST_GROUP[q] + 4, W_READY + b)
 
-        for step in range(GROUPS + BATCH):
-            bank, second = divmod(step - 2, BANK_HEADS // GROUP)
-            divides = second == 1 and 0 <= bank < ALL_HEADS // BANK_HEADS
+        def square_step(b):
+            return project_step(PASSES * b + PASSES - 1) + (3 if b == BATCH - 2 else 1)
 
+        waiting = [part for b in range(BATCH - 1) for part in layer_norm_parts(b)]
+
+        def use_wait(first, count):
+            for part in waiting[first : first + count]:
+                part()
+
+        for step in range(GROUPS + 4):
+            ready = step - 2
+            start, end = divided_heads(ready) if 0 <= ready < GROUPS else (0, 0)
+
+            if step == W_FIRST_STEP - 1:
+                make_hidden()
+            if step == GROUPS - 1:
+                sum_by_tensor(step)
             if step < GROUPS:
                 add_scores(step)
             for r in range(W_ROWS):
                 if step == W_FIRST_STEP + r // W_PER_STEP + 1:
                     quantise_w(r)
-            for b in range(BATCH):
-                if step == turn_step(b) + 1:
-                    c_grouped_of[b] = double.tile([P, PASSES, P, PACK], BF16, name="c_grouped", align_bytes=64)
-                    copy_words(c_words_of[b], c_grouped_of[b])
-                    project(b)
+            for q in range(BANKS):
+                if step == LAST_GROUP[q] + 4:
+                    quantise_c(q)
             if 0 <= step - 1 < GROUPS:
                 exponentials(step - 1)
+            for q in range(BANKS):
+                if step == LAST_GROUP[q] + 3:
+                    turn_c(q)
             if step < GROUPS:
                 regroup_values(step)
+            for q in range(BANKS):
+                if step == LAST_GROUP[q] + 3:
+                    copy_c(q)
+            for b in range(BATCH - 1):
+                if step == square_step(b):
+                    square(b)
             for r in range(W_ROWS):
                 if step == W_FIRST_STEP + r // W_PER_STEP:
                     turn_w(r)
-            if 0 <= step - 2 < GROUPS:
-                quantise_group(step - 2)
-                attend(step - 2)
-            if divides:
-                invert_rowsums(bank)
+            if 0 <= ready < GROUPS:
+                quantise_group(ready)
+                attend(ready)
+            for q in range(BANKS):
+                if step == project_step(q):
+                    project(q)
+            if step == GROUPS - 3:
+                sum_by_tensor(GROUPS - 2)
+            if step == GROUPS:
+                use_wait(4, 3)
+            if step == GROUPS + 1:
+                use_wait(7, 1)
+            invert_rowsums(start, end)
 
             if step + LOAD_BUFS < GROUPS:
-                load_group(step + LOAD_BUFS)
+                load_scores(step + LOAD_BUFS)
+                load_values(step + LOAD_BUFS)
             if step < 2:
                 rows = slice(step * W_ROWS // 2, (step + 1) * W_ROWS // 2)
                 nc.sync.dma_start(out=w_raw[:, rows, :], in_=w_view[:, rows, :])
@@ -345,16 +504,23 @@ def tile_maskedmultiheadattention_pa_kernel(
                 nc.sync.dma_start(out=gain[:], in_=ln_w.partition_broadcast(P))
                 nc.sync.dma_start(out=bias[:], in_=ln_b.partition_broadcast(P))
 
+            if GROUPS - 4 <= step < GROUPS:
+                use_wait(step - (GROUPS - 4), 1)
             if step + 1 < GROUPS:
                 hide(step + 1)
             if step < GROUPS:
                 row_maxima(step)
-            if divides:
-                divide(bank)
+            divide(start, end)
+            if step == GROUPS + 1:
+                use_wait(8, 2)
+            if step == GROUPS + 3:
+                use_wait(10, 2)
             for b in range(BATCH):
-                if step == turn_step(b):
-                    c_words_of[b] = transpose_words(c_of[b][:].rearrange("p n i -> p (n i)"))
-                if step == turn_step(b) + 1:
+                if step == project_step(PASSES * b + PASSES - 1):
                     add_residual(b)
-            if step >= GROUPS:
-                layer_norm(step - GROUPS)
+                    if b < BATCH - 1:
+                        find_mean(b)
+                if b < BATCH - 1 and step == square_step(b) + 1:
+                    find_rstd(b)
+        for part in layer_norm_parts(BATCH - 1):
+            part()

@@ -79,6 +79,10 @@ def tile_maskedmultiheadattention_pa_kernel(
         make_identity(nc, identity_bf16[:])
         minus_half = const.tile([P, 1], F32)
         nc.vector.memset(minus_half[:], -0.5)
+        eps = const.tile([P, 1], F32)
+        nc.vector.tensor_scalar(
+            out=eps[:], in0=minus_half[:], scalar1=0.0, scalar2=LN_EPS, op0=ALU.mult, op1=ALU.add
+        )
         table_warmer = const.tile([P, 1], F32)
         nc.scalar.activation(out=table_warmer[:], in_=minus_half[:], func=ACT.Exp)
         cap = const.tile([P, WINDOW], BF16)
@@ -118,7 +122,7 @@ def tile_maskedmultiheadattention_pa_kernel(
                 return KEYS
             if GROUP_SIZES[g] == 2:
                 return KEYS
-            return 2 * KEYS if (g - 3) in LAST_GROUP else 5 * KEYS // 2
+            return 1280 if (g - 3) in LAST_GROUP else 1536
 
         def load_scores(g):
             n, size = FIRST_HEAD[g], GROUP_SIZES[g]
@@ -196,7 +200,7 @@ def tile_maskedmultiheadattention_pa_kernel(
                 return
             nc.vector.tensor_reduce(out=top_of[g][:], in_=sum_of[g][:], axis=AXIS_X, op=ALU.max)
 
-        def exponentials(g):
+        def exponentials(g, between):
             size = GROUP_SIZES[g]
             shift = double.tile([P, size], F32, name="shift")
             nc.scalar.mul(out=shift[:], in_=top_of[g][:], mul=-SCALE)
@@ -211,15 +215,19 @@ def tile_maskedmultiheadattention_pa_kernel(
                     accum_out=rowsum[:, n : n + 1],
                 )
             e_grouped_of[g] = triple.tile([P, size, P, PACK], BF16, name="e_grouped", align_bytes=64)
+            turned = []
             for first in range(0, size, 2):
                 pair = range(first, min(first + 2, size))
                 e_t = psum.tile([P, len(pair), 2, P], F32, name="e_t")
+                turned.append((first, e_t))
                 for k in pair:
                     e_words = e[:, k, :].bitcast(F32)
                     for u in range(2):
                         nc.tensor.transpose(e_t[:, k - first, u, :], e_words[:, u : 2 * P : 2], identity[:])
+            between()
+            for first, e_t in turned:
                 nc.scalar.copy(
-                    out=e_grouped_of[g][:, first : first + len(pair), :, :].bitcast(F32),
+                    out=e_grouped_of[g][:, first : min(first + 2, size), :, :].bitcast(F32),
                     in_=e_t[:].rearrange("p k u s -> p k s u"),
                 )
 
@@ -304,21 +312,23 @@ def tile_maskedmultiheadattention_pa_kernel(
             return turned
 
         def copy_words(turned, grouped):
-            nc.scalar.copy(out=grouped[:].bitcast(F32), in_=turned[:].rearrange("p (g u) r -> p g r u", u=2))
+            nc.scalar.copy(out=grouped.bitcast(F32), in_=turned[:].rearrange("p (g u) r -> p g r u", u=2))
 
-        def turn_w(r):
-            w_grouped_of[r] = double.tile(
-                [P, PASSES, P, PACK], BF16, name="w_grouped", bufs=2 * W_PER_STEP, align_bytes=64
-            )
-            copy_words(transpose_words(w_raw[:, r, :], PASSES), w_grouped_of[r])
+        def turn_w(i):
+            w_grouped_of[i] = double.tile([P, PASSES, W_PER_STEP * P, PACK], BF16, name="w_grouped", align_bytes=64)
+            for r in range(W_PER_STEP):
+                copy_words(
+                    transpose_words(w_raw[:, i * W_PER_STEP + r, :], PASSES),
+                    w_grouped_of[i][:, :, r * P : (r + 1) * P, :],
+                )
 
-        def quantise_w(r):
-            rows = slice(r * P, (r + 1) * P)
+        def quantise_w(i):
+            rows = slice(i * W_PER_STEP * P, (i + 1) * W_PER_STEP * P)
             for g in range(PASSES):
                 nc.vector.quantize_mx(
                     out=w_codes[:, g, rows].bitcast(FP8X4),
                     scales=w_scales[:, g, rows],
-                    in_=w_grouped_of[r][:, g, :, :].rearrange("p r t -> p (r t)"),
+                    in_=w_grouped_of[i][:, g, :, :].rearrange("p r t -> p (r t)"),
                 )
 
         def turn_c(q):
@@ -326,7 +336,7 @@ def tile_maskedmultiheadattention_pa_kernel(
 
         def copy_c(q):
             c_grouped_of[q] = double.tile([P, 1, P, PACK], BF16, name="c_grouped", align_bytes=64)
-            copy_words(c_words_of[q], c_grouped_of[q])
+            copy_words(c_words_of[q], c_grouped_of[q][:])
 
         def quantise_c(q):
             c_codes_of[q] = double.tile([P, P], U32, name="c_codes", bufs=4, align_bytes=64)
@@ -377,17 +387,17 @@ def tile_maskedmultiheadattention_pa_kernel(
             nc.vector.bn_aggr(out=moments[:], in_=stats[:].rearrange("p c k -> p (c k)"))
             mean_of[b] = moments[:, 0:1]
             spread = double.tile([P, 1], F32, name="spread")
-            nc.gpsimd.tensor_scalar_add(out=spread[:], in0=moments[:, 1:2], scalar1=LN_EPS)
+            nc.scalar.activation(out=spread[:], in_=moments[:, 1:2], func=ACT.Identity, bias=eps[:])
             rstd_of[b] = const.tile([P, 1], F32, name="rstd_%d" % b)
             nc.gpsimd.tensor_tensor(out=rstd_of[b][:], in0=spread[:], in1=minus_half[:], op=ALU.pow)
 
         def find_mean(b):
             total = double.tile([P, 1], F32, name="total")
-            nc.gpsimd.tensor_tensor(out=total[:], in0=sums_of[b][:, 0:1], in1=sums_of[b][:, 1:2], op=ALU.add)
-            mean = const.tile([P, 1], F32, name="mean_%d" % b)
-            nc.gpsimd.tensor_scalar(
-                out=mean[:], in0=total[:], scalar1=1.0 / FEATURES, scalar2=0.0, op0=ALU.mult, op1=ALU.add
+            nc.scalar.activation(
+                out=total[:], in_=sums_of[b][:, 0:1], func=ACT.Identity, bias=sums_of[b][:, 1:2]
             )
+            mean = const.tile([P, 1], F32, name="mean_%d" % b)
+            nc.scalar.mul(out=mean[:], in_=total[:], mul=1.0 / FEATURES)
             mean_of[b] = mean[:]
 
         def square(b):
@@ -396,15 +406,18 @@ def tile_maskedmultiheadattention_pa_kernel(
             nc.scalar.activation(out=squares[:], in_=o_of[b][:], func=ACT.Square, accum_out=square_sum_of[b][:])
 
         def find_rstd(b):
-            work = double.tile([P, 3], F32, name="work")
-            nc.gpsimd.tensor_tensor(out=work[:, 0:1], in0=mean_of[b], in1=mean_of[b], op=ALU.mult)
-            nc.gpsimd.tensor_scalar(
-                out=work[:, 1:2], in0=square_sum_of[b][:], scalar1=1.0 / FEATURES, scalar2=LN_EPS,
-                op0=ALU.mult, op1=ALU.add,
+            mean_square = double.tile([P, 1], F32, name="mean_square")
+            nc.scalar.activation(out=mean_square[:], in_=mean_of[b], func=ACT.Square)
+            spread = double.tile([P, 1], F32, name="spread")
+            nc.scalar.activation(
+                out=spread[:], in_=square_sum_of[b][:], func=ACT.Identity, scale=1.0 / FEATURES, bias=eps[:]
             )
-            nc.gpsimd.tensor_tensor(out=work[:, 2:3], in0=work[:, 1:2], in1=work[:, 0:1], op=ALU.subtract)
+            spread_less = double.tile([P, 1], F32, name="spread_less")
+            nc.scalar.activation(
+                out=spread_less[:], in_=mean_square[:], func=ACT.Identity, scale=-1.0, bias=spread[:]
+            )
             rstd_of[b] = const.tile([P, 1], F32, name="rstd_%d" % b)
-            nc.gpsimd.tensor_tensor(out=rstd_of[b][:], in0=work[:, 2:3], in1=minus_half[:], op=ALU.pow)
+            nc.gpsimd.tensor_tensor(out=rstd_of[b][:], in0=spread_less[:], in1=minus_half[:], op=ALU.pow)
 
         def layer_norm_parts(b):
             def centre(half):
@@ -456,28 +469,32 @@ def tile_maskedmultiheadattention_pa_kernel(
                 sum_by_tensor(step)
             if step < GROUPS:
                 add_scores(step)
-            for r in range(W_ROWS):
-                if step == W_FIRST_STEP + r // W_PER_STEP + 1:
-                    quantise_w(r)
+            if W_FIRST_STEP < step <= W_READY:
+                quantise_w(step - W_FIRST_STEP - 1)
             for q in range(BANKS):
                 if step == LAST_GROUP[q] + 4:
                     quantise_c(q)
+            def regroup_now():
+                if step < GROUPS:
+                    regroup_values(step)
+
             if 0 <= step - 1 < GROUPS:
-                exponentials(step - 1)
+                exponentials(step - 1, regroup_now)
+            else:
+                regroup_now()
             for q in range(BANKS):
                 if step == LAST_GROUP[q] + 3:
                     turn_c(q)
-            if step < GROUPS:
-                regroup_values(step)
             for q in range(BANKS):
                 if step == LAST_GROUP[q] + 3:
                     copy_c(q)
             for b in range(BATCH - 1):
+                if step == project_step(PASSES * b + PASSES - 1) + 1:
+                    find_mean(b)
                 if step == square_step(b):
                     square(b)
-            for r in range(W_ROWS):
-                if step == W_FIRST_STEP + r // W_PER_STEP:
-                    turn_w(r)
+            if W_FIRST_STEP <= step < W_READY:
+                turn_w(step - W_FIRST_STEP)
             if 0 <= ready < GROUPS:
                 quantise_group(ready)
                 attend(ready)
@@ -518,8 +535,6 @@ def tile_maskedmultiheadattention_pa_kernel(
             for b in range(BATCH):
                 if step == project_step(PASSES * b + PASSES - 1):
                     add_residual(b)
-                    if b < BATCH - 1:
-                        find_mean(b)
                 if b < BATCH - 1 and step == square_step(b) + 1:
                     find_rstd(b)
         for part in layer_norm_parts(BATCH - 1):

@@ -31,18 +31,20 @@ WINDOW = P
 OPEN_KEYS = KEYS - WINDOW
 HIDDEN = 1e30
 
-GROUP_SIZES = (1, 1, 2) + 14 * (4,) + (2, 2)
+GROUP_SIZES = 15 * (4,) + (2, 2)
+FIRST_LOADS = ((0, 1), (1, 2), (2, 4))
 GROUPS = len(GROUP_SIZES)
 FIRST_HEAD = [sum(GROUP_SIZES[:g]) for g in range(GROUPS)]
 MAX_GROUP = 4
+LEADERS = range(1, GROUPS - 1, 2)
 BANK_HEADS = N_TILE // WIDTH
 BANKS = ALL_HEADS // BANK_HEADS
 LAST_GROUP = [max(g for g in range(GROUPS) if FIRST_HEAD[g] < (q + 1) * BANK_HEADS) for q in range(BANKS)]
-LOAD_BUFS = 6
-SUMMED_BY_TENSOR = (GROUPS - 2, GROUPS - 1)
+LOAD_BUFS = 5
+SUMMED_BY_TENSOR = (1,)
 RUN = 4
 W_ROWS = FEATURES // P
-W_FIRST_STEP = 6
+W_FIRST_STEP = 5
 W_PER_STEP = 2
 W_READY = W_FIRST_STEP + W_ROWS // W_PER_STEP
 
@@ -99,8 +101,6 @@ def tile_maskedmultiheadattention_pa_kernel(
 
         rowsum = const.tile([P, ALL_HEADS], F32)
         inverse = const.tile([P, ALL_HEADS], F32)
-        v_codes = const.tile([P, ALL_HEADS * WIDTH], U32, align_bytes=64)
-        v_scales = const.tile([P, ALL_HEADS * WIDTH], U8, align_bytes=64)
         w_raw = const.tile([P, W_ROWS, FEATURES], BF16)
         w_codes = const.tile([P, PASSES, FEATURES], U32, align_bytes=64)
         w_scales = const.tile([P, PASSES, FEATURES], U8, align_bytes=64)
@@ -108,8 +108,8 @@ def tile_maskedmultiheadattention_pa_kernel(
         gain = const.tile([P, FEATURES], BF16)
         bias = const.tile([P, FEATURES], BF16)
 
-        head_sums_of = {}
-        content_of, pos_of, v_raw_of, sum_of, top_of, e_grouped_of = {}, {}, {}, {}, {}, {}
+        head_sums_of, grouped_of, v_place_of = {}, {}, {}
+        content_of, pos_of, v_raw_of, sum_of, top_of = {}, {}, {}, {}, {}
         e_codes_of, e_scales_of, v_grouped_of, ctx_bank_of = {}, {}, {}, {}
         w_grouped_of, c_of, c_words_of, c_grouped_of, c_codes_of, c_scales_of = {}, {}, {}, {}, {}, {}
         o_banks_of, o_of, mean_of, rstd_of, sums_of, square_sum_of = {}, {}, {}, {}, {}, {}
@@ -118,20 +118,24 @@ def tile_maskedmultiheadattention_pa_kernel(
             return range(FIRST_HEAD[g], FIRST_HEAD[g] + GROUP_SIZES[g])
 
         def vector_columns(g):
-            if GROUP_SIZES[g] == 1:
-                return KEYS
-            if GROUP_SIZES[g] == 2:
-                return KEYS
-            return 1280 if (g - 3) in LAST_GROUP else 1536
+            columns = GROUP_SIZES[g] * KEYS
+            if g < 3:
+                return columns
+            share = GROUP_SIZES[g - 1] * KEYS // 4
+            if g - 3 in LAST_GROUP:
+                share += KEYS // 1
+            return columns - min(columns, share)
 
         def load_scores(g):
             n, size = FIRST_HEAD[g], GROUP_SIZES[g]
-            heads = slice(n, n + size)
             pos_of[g] = loaded.tile([P, size, KEYS], BF16, name="pos")
-            nc.sync.dma_start(out=pos_of[g][:, :, OPEN_KEYS:KEYS], in_=pos_from_1[:, heads, OPEN_KEYS - 1 : KEYS - 1])
-            nc.sync.dma_start(out=pos_of[g][:, :, 0:OPEN_KEYS], in_=pos_from_0[:, heads, 0:OPEN_KEYS])
             content_of[g] = loaded.tile([P, size, KEYS], BF16, name="content")
-            nc.sync.dma_start(out=content_of[g][:], in_=content_view[:, heads, :])
+            for start, end in FIRST_LOADS if g == 0 else ((0, size),):
+                places, heads = slice(start, end), slice(n + start, n + end)
+                window = pos_of[g][:, places, OPEN_KEYS:KEYS]
+                nc.sync.dma_start(out=window, in_=pos_from_1[:, heads, OPEN_KEYS - 1 : KEYS - 1])
+                nc.sync.dma_start(out=pos_of[g][:, places, 0:OPEN_KEYS], in_=pos_from_0[:, heads, 0:OPEN_KEYS])
+                nc.sync.dma_start(out=content_of[g][:, places, :], in_=content_view[:, heads, :])
 
         def load_values(g):
             n, size = FIRST_HEAD[g], GROUP_SIZES[g]
@@ -163,6 +167,21 @@ def tile_maskedmultiheadattention_pa_kernel(
                     op=ALU.add,
                 )
 
+        def first_group():
+            sum_of[0] = triple.tile([P, GROUP_SIZES[0], KEYS], F32, name="score_sum")
+            head_sums_of[0] = [sum_of[0][:, k, :] for k in range(GROUP_SIZES[0])]
+            top_of[0] = triple.tile([P, GROUP_SIZES[0]], F32, name="top")
+            for start, end in FIRST_LOADS:
+                heads = slice(start, end)
+                window = pos_of[0][:, heads, OPEN_KEYS:KEYS]
+                nc.vector.tensor_tensor(
+                    out=window, in0=window, in1=cap[:].unsqueeze(1).to_broadcast([P, end - start, WINDOW]), op=ALU.min
+                )
+                nc.vector.tensor_tensor(
+                    out=sum_of[0][:, heads, :], in0=content_of[0][:, heads, :], in1=pos_of[0][:, heads, :], op=ALU.add
+                )
+                nc.vector.tensor_reduce(out=top_of[0][:, heads], in_=sum_of[0][:, heads, :], axis=AXIS_X, op=ALU.max)
+
         def add_scores(g):
             if g in SUMMED_BY_TENSOR:
                 return
@@ -174,10 +193,9 @@ def tile_maskedmultiheadattention_pa_kernel(
                 op=ALU.add,
             )
 
-        def sum_by_tensor(g):
-            head_sums_of[g] = []
-            for k in range(GROUP_SIZES[g]):
-                if g == GROUPS - 1:
+        def sum_by_tensor(g, places):
+            for k in places:
+                if k >= 2:
                     head_sum = psum.tile([P, KEYS], F32, name="o_bank")
                 else:
                     head_sum = psum.tile([P, KEYS], F32, name="turned")
@@ -188,7 +206,7 @@ def tile_maskedmultiheadattention_pa_kernel(
                     head_sum[:, OPEN_KEYS:KEYS], lhsT=identity_bf16[:], rhs=hidden[:], start=False, stop=False
                 )
                 nc.tensor.matmul(head_sum[:], lhsT=identity_bf16[:], rhs=pos_of[g][:, k, :], start=False, stop=True)
-                head_sums_of[g].append(head_sum[:])
+                head_sums_of.setdefault(g, []).append(head_sum[:])
 
         def row_maxima(g):
             top_of[g] = triple.tile([P, GROUP_SIZES[g]], F32, name="top")
@@ -203,9 +221,17 @@ def tile_maskedmultiheadattention_pa_kernel(
         def exponentials(g, between):
             size = GROUP_SIZES[g]
             shift = double.tile([P, size], F32, name="shift")
-            nc.scalar.mul(out=shift[:], in_=top_of[g][:], mul=-SCALE)
+            if g == 0:
+                found_together = FIRST_LOADS
+            elif g in SUMMED_BY_TENSOR:
+                found_together = [(k, k + 1) for k in range(size)]
+            else:
+                found_together = ((0, size),)
             e = double.tile([P, size, KEYS], BF16, name="e")
             for k, n in enumerate(heads_of(g)):
+                for start, end in found_together:
+                    if k == start:
+                        nc.scalar.mul(out=shift[:, start:end], in_=top_of[g][:, start:end], mul=-SCALE)
                 nc.scalar.activation(
                     out=e[:, k, :],
                     in_=head_sums_of[g][k],
@@ -214,7 +240,8 @@ def tile_maskedmultiheadattention_pa_kernel(
                     scale=SCALE,
                     accum_out=rowsum[:, n : n + 1],
                 )
-            e_grouped_of[g] = triple.tile([P, size, P, PACK], BF16, name="e_grouped", align_bytes=64)
+            if g not in grouped_of:
+                grouped_of[g] = double.tile([P, size * KEYS], BF16, name="e_grouped", align_bytes=64)
             turned = []
             for first in range(0, size, 2):
                 pair = range(first, min(first + 2, size))
@@ -224,37 +251,55 @@ def tile_maskedmultiheadattention_pa_kernel(
                     e_words = e[:, k, :].bitcast(F32)
                     for u in range(2):
                         nc.tensor.transpose(e_t[:, k - first, u, :], e_words[:, u : 2 * P : 2], identity[:])
+                if g + 1 in SUMMED_BY_TENSOR:
+                    sum_by_tensor(g + 1, pair)
             between()
             for first, e_t in turned:
+                pair = grouped_of[g][:, first * KEYS : min(first + 2, size) * KEYS].bitcast(F32)
                 nc.scalar.copy(
-                    out=e_grouped_of[g][:, first : min(first + 2, size), :, :].bitcast(F32),
-                    in_=e_t[:].rearrange("p k u s -> p k s u"),
+                    out=pair.rearrange("p (k r u) -> p k r u", r=P, u=2), in_=e_t[:].rearrange("p k u r -> p k r u")
                 )
 
         def regroup_values(g):
             size = GROUP_SIZES[g]
-            v_grouped_of[g] = triple.tile([P, size, WIDTH, PACK], BF16, name="v_grouped", align_bytes=64)
+            if g in LEADERS:
+                width = size * KEYS + (size + GROUP_SIZES[g + 1]) * WIDTH * PACK
+                grouped_of[g] = triple.tile([P, width], BF16, name="grouped", align_bytes=64)
+                home, start = grouped_of[g], size * KEYS
+            elif g - 1 in LEADERS:
+                home, start = grouped_of[g - 1], GROUP_SIZES[g - 1] * (KEYS + WIDTH * PACK)
+            else:
+                v_grouped_of[g] = double.tile([P, size * WIDTH * PACK], BF16, name="v_grouped", align_bytes=64)
+                home, start = v_grouped_of[g], 0
             for k in range(size):
+                first = start + k * WIDTH * PACK
                 nc.scalar.copy(
-                    out=v_grouped_of[g][:, k, :, :].rearrange("p (c i) t -> p c t i", i=RUN),
+                    out=home[:, first : first + WIDTH * PACK].rearrange("p (c i t) -> p c t i", i=RUN, t=PACK),
                     in_=v_raw_of[g][:, k, :, :].rearrange("p t (c i) -> p c t i", i=RUN),
                 )
 
         def quantise_group(g):
             size = GROUP_SIZES[g]
-            e_codes_of[g] = double.tile([P, size * P], U32, name="e_codes", align_bytes=64)
-            e_scales_of[g] = double.tile([P, size * P], U8, name="e_scales", align_bytes=64)
-            nc.vector.quantize_mx(
-                out=e_codes_of[g][:].bitcast(FP8X4),
-                scales=e_scales_of[g][:],
-                in_=e_grouped_of[g][:].rearrange("p k s t -> p (k s t)"),
-            )
-            columns = slice(FIRST_HEAD[g] * WIDTH, (FIRST_HEAD[g] + size) * WIDTH)
-            nc.vector.quantize_mx(
-                out=v_codes[:, columns].bitcast(FP8X4),
-                scales=v_scales[:, columns],
-                in_=v_grouped_of[g][:].rearrange("p n i t -> p (n i t)"),
-            )
+            width = size * P
+            if g in LEADERS:
+                width += (size + GROUP_SIZES[g + 1]) * WIDTH
+                codes = double.tile([P, width], U32, name="codes", align_bytes=64)
+                scales = double.tile([P, width], U8, name="scales", align_bytes=64)
+                for n in heads_of(g):
+                    v_place_of[n] = codes, scales, size * P + (n - FIRST_HEAD[g]) * WIDTH
+                for n in heads_of(g + 1):
+                    v_place_of[n] = codes, scales, size * P + (n - FIRST_HEAD[g]) * WIDTH
+            else:
+                codes = double.tile([P, width], U32, name="e_codes", align_bytes=64)
+                scales = double.tile([P, width], U8, name="e_scales", align_bytes=64)
+            e_codes_of[g], e_scales_of[g] = codes, scales
+            nc.vector.quantize_mx(out=codes[:].bitcast(FP8X4), scales=scales[:], in_=grouped_of[g][:])
+            if g in v_grouped_of:
+                codes = double.tile([P, size * WIDTH], U32, name="v_codes", align_bytes=64)
+                scales = double.tile([P, size * WIDTH], U8, name="v_scales", align_bytes=64)
+                for n in heads_of(g):
+                    v_place_of[n] = codes, scales, (n - FIRST_HEAD[g]) * WIDTH
+                nc.vector.quantize_mx(out=codes[:].bitcast(FP8X4), scales=scales[:], in_=v_grouped_of[g][:])
 
         def attend(g):
             for k, n in enumerate(heads_of(g)):
@@ -262,7 +307,8 @@ def tile_maskedmultiheadattention_pa_kernel(
                 if place == 0:
                     ctx_bank_of[bank] = psum.tile([P, BANK_HEADS, WIDTH], F32, name="ctx_bank")
                 queries = slice(k * P, (k + 1) * P)
-                features = slice(n * WIDTH, (n + 1) * WIDTH)
+                v_codes, v_scales, first = v_place_of[n]
+                features = slice(first, first + WIDTH)
                 nc.tensor.matmul_mx(
                     out=ctx_bank_of[bank][:, place, :],
                     lhsT=e_codes_of[g][:, queries].bitcast(FP8X4),
@@ -335,28 +381,32 @@ def tile_maskedmultiheadattention_pa_kernel(
             c_words_of[q] = transpose_words(c_of[q][:].rearrange("p n i -> p (n i)"), 1)
 
         def copy_c(q):
-            c_grouped_of[q] = double.tile([P, 1, P, PACK], BF16, name="c_grouped", align_bytes=64)
-            copy_words(c_words_of[q], c_grouped_of[q][:])
+            b, g = divmod(q, PASSES)
+            if g == 0:
+                c_grouped_of[b] = double.tile([P, PASSES, P, PACK], BF16, name="c_grouped", align_bytes=64)
+                c_codes_of[b] = double.tile([P, PASSES * P], U32, name="c_codes", align_bytes=64)
+                c_scales_of[b] = double.tile([P, PASSES * P], U8, name="c_scales", align_bytes=64)
+            copy_words(c_words_of[q], c_grouped_of[b][:, g : g + 1, :, :])
 
-        def quantise_c(q):
-            c_codes_of[q] = double.tile([P, P], U32, name="c_codes", bufs=4, align_bytes=64)
-            c_scales_of[q] = double.tile([P, P], U8, name="c_scales", bufs=4, align_bytes=64)
+        def quantise_c(b, passes):
+            columns = slice(passes[0] * P, (passes[-1] + 1) * P)
             nc.vector.quantize_mx(
-                out=c_codes_of[q][:].bitcast(FP8X4),
-                scales=c_scales_of[q][:],
-                in_=c_grouped_of[q][:].rearrange("p g s t -> p (g s t)"),
+                out=c_codes_of[b][:, columns].bitcast(FP8X4),
+                scales=c_scales_of[b][:, columns],
+                in_=c_grouped_of[b][:, passes[0] : passes[-1] + 1, :, :].rearrange("p g s t -> p (g s t)"),
             )
 
         def project(q):
             b, g = divmod(q, PASSES)
+            queries = slice(g * P, (g + 1) * P)
             if g == 0:
                 o_banks_of[b] = [psum.tile([P, N_TILE], F32, name="o_bank") for half in range(HALVES)]
             for half in range(HALVES):
                 outputs = slice(half * N_TILE, (half + 1) * N_TILE)
                 nc.tensor.matmul_mx(
                     out=o_banks_of[b][half][:],
-                    lhsT=c_codes_of[q][:].bitcast(FP8X4),
-                    lhsT_scale=c_scales_of[q][:],
+                    lhsT=c_codes_of[b][:, queries].bitcast(FP8X4),
+                    lhsT_scale=c_scales_of[b][:, queries],
                     rhs=w_codes[:, g, outputs].bitcast(FP8X4),
                     rhs_scale=w_scales[:, g, outputs],
                     start=(g == 0),
@@ -437,23 +487,38 @@ def tile_maskedmultiheadattention_pa_kernel(
 
             return [lambda: centre(0), lambda: centre(1), lambda: finish(0), lambda: finish(1)]
 
-        for g in range(3):
+        def layer_norm_rows(b):
+            def centre():
+                nc.vector.scalar_tensor_tensor(
+                    out=o_of[b][:], in0=o_of[b][:], scalar=mean_of[b], in1=gain[:], op0=ALU.subtract, op1=ALU.mult
+                )
+
+            def finish():
+                nc.vector.scalar_tensor_tensor(
+                    out=o_of[b][:], in0=o_of[b][:], scalar=rstd_of[b][:, 0:1], in1=bias[:], op0=ALU.mult, op1=ALU.add
+                )
+                nc.sync.dma_start(out=out[:, b, :], in_=o_of[b][:])
+
+            return [centre, finish]
+
+        load_scores(0)
+        for g in range(1, LOAD_BUFS):
             load_scores(g)
-        for g in range(3):
-            load_values(g)
-        for g in range(3, LOAD_BUFS):
-            load_scores(g)
-            load_values(g)
-        hide(0)
+            load_values(g - 1)
+        load_values(LOAD_BUFS - 1)
+        first_group()
+        make_hidden()
 
         def project_step(q):
             b, g = divmod(q, PASSES)
-            return max(LAST_GROUP[q] + 4, W_READY + b)
+            if b < BATCH - 1:
+                return max(LAST_GROUP[PASSES * b + 1] + 4, W_READY + b)
+            return LAST_GROUP[q] + 4
 
         def square_step(b):
             return project_step(PASSES * b + PASSES - 1) + (3 if b == BATCH - 2 else 1)
 
-        waiting = [part for b in range(BATCH - 1) for part in layer_norm_parts(b)]
+        waiting = layer_norm_rows(0) + layer_norm_rows(1) + layer_norm_rows(2)
 
         def use_wait(first, count):
             for part in waiting[first : first + count]:
@@ -463,22 +528,22 @@ def tile_maskedmultiheadattention_pa_kernel(
             ready = step - 2
             start, end = divided_heads(ready) if 0 <= ready < GROUPS else (0, 0)
 
-            if step == W_FIRST_STEP - 1:
-                make_hidden()
-            if step == GROUPS - 1:
-                sum_by_tensor(step)
-            if step < GROUPS:
+            if 0 < step < GROUPS:
                 add_scores(step)
             if W_FIRST_STEP < step <= W_READY:
                 quantise_w(step - W_FIRST_STEP - 1)
-            for q in range(BANKS):
-                if step == LAST_GROUP[q] + 4:
-                    quantise_c(q)
+            for b in range(BATCH):
+                if b == BATCH - 1 and step == LAST_GROUP[PASSES * b] + 4:
+                    quantise_c(b, (0,))
+                if step == LAST_GROUP[PASSES * b + 1] + 4:
+                    quantise_c(b, (1,) if b == BATCH - 1 else (0, 1))
             def regroup_now():
-                if step < GROUPS:
+                if 0 < step < GROUPS:
                     regroup_values(step)
 
-            if 0 <= step - 1 < GROUPS:
+            if step == 0:
+                exponentials(0, lambda: regroup_values(0))
+            elif 0 < step - 1 < GROUPS:
                 exponentials(step - 1, regroup_now)
             else:
                 regroup_now()
@@ -501,12 +566,8 @@ def tile_maskedmultiheadattention_pa_kernel(
             for q in range(BANKS):
                 if step == project_step(q):
                     project(q)
-            if step == GROUPS - 3:
-                sum_by_tensor(GROUPS - 2)
             if step == GROUPS:
-                use_wait(4, 3)
-            if step == GROUPS + 1:
-                use_wait(7, 1)
+                use_wait(2, 2)
             invert_rowsums(start, end)
 
             if step + LOAD_BUFS < GROUPS:
@@ -521,17 +582,19 @@ def tile_maskedmultiheadattention_pa_kernel(
                 nc.sync.dma_start(out=gain[:], in_=ln_w.partition_broadcast(P))
                 nc.sync.dma_start(out=bias[:], in_=ln_b.partition_broadcast(P))
 
-            if GROUPS - 4 <= step < GROUPS:
-                use_wait(step - (GROUPS - 4), 1)
+            if GROUPS - 2 <= step < GROUPS:
+                use_wait(step - (GROUPS - 2), 1)
+            if step == 1:
+                row_maxima(1)
             if step + 1 < GROUPS:
                 hide(step + 1)
-            if step < GROUPS:
+            if 1 < step < GROUPS:
                 row_maxima(step)
             divide(start, end)
             if step == GROUPS + 1:
-                use_wait(8, 2)
+                use_wait(4, 1)
             if step == GROUPS + 3:
-                use_wait(10, 2)
+                use_wait(5, 1)
             for b in range(BATCH):
                 if step == project_step(PASSES * b + PASSES - 1):
                     add_residual(b)

@@ -41,7 +41,8 @@ BANK_HEADS = N_TILE // WIDTH
 BANKS = ALL_HEADS // BANK_HEADS
 LAST_GROUP = [max(g for g in range(GROUPS) if FIRST_HEAD[g] < (q + 1) * BANK_HEADS) for q in range(BANKS)]
 LOAD_BUFS = 5
-SUMMED_BY_TENSOR = (1,)
+SUMMED_BY_TENSOR = (2, 3)
+SUMMED_HEADS = 2
 RUN = 4
 W_ROWS = FEATURES // P
 W_FIRST_STEP = 5
@@ -121,10 +122,10 @@ def tile_maskedmultiheadattention_pa_kernel(
             columns = GROUP_SIZES[g] * KEYS
             if g < 3:
                 return columns
-            share = GROUP_SIZES[g - 1] * KEYS // 4
+            share = GROUP_SIZES[g - 1] * 640 // 4
             if g - 3 in LAST_GROUP:
-                share += KEYS // 1
-            return columns - min(columns, share)
+                share += 512
+            return columns - min(columns - summed_heads(g) * KEYS, share)
 
         def load_scores(g):
             n, size = FIRST_HEAD[g], GROUP_SIZES[g]
@@ -148,15 +149,14 @@ def tile_maskedmultiheadattention_pa_kernel(
             return tile[:].rearrange("p n j -> p (n j)")
 
         def hide(g):
-            if g in SUMMED_BY_TENSOR:
-                return
-            size = GROUP_SIZES[g]
-            window = pos_of[g][:, :, OPEN_KEYS:KEYS]
+            size, summed = GROUP_SIZES[g], summed_heads(g)
+            window = pos_of[g][:, summed:size, OPEN_KEYS:KEYS]
             nc.vector.tensor_tensor(
-                out=window, in0=window, in1=cap[:].unsqueeze(1).to_broadcast([P, size, WINDOW]), op=ALU.min
+                out=window, in0=window, in1=cap[:].unsqueeze(1).to_broadcast([P, size - summed, WINDOW]), op=ALU.min
             )
             sum_of[g] = triple.tile([P, size, KEYS], F32, name="score_sum")
-            head_sums_of[g] = [sum_of[g][:, k, :] for k in range(size)]
+            for k in range(summed, size):
+                head_sums_of.setdefault(g, []).append(sum_of[g][:, k, :])
             first = vector_columns(g)
             if first < size * KEYS:
                 columns = slice(first, size * KEYS)
@@ -183,9 +183,9 @@ def tile_maskedmultiheadattention_pa_kernel(
                 nc.vector.tensor_reduce(out=top_of[0][:, heads], in_=sum_of[0][:, heads, :], axis=AXIS_X, op=ALU.max)
 
         def add_scores(g):
-            if g in SUMMED_BY_TENSOR:
+            columns = slice(summed_heads(g) * KEYS, vector_columns(g))
+            if columns.start == columns.stop:
                 return
-            columns = slice(0, vector_columns(g))
             nc.vector.tensor_tensor(
                 out=flat(sum_of[g])[:, columns],
                 in0=flat(content_of[g])[:, columns],
@@ -193,9 +193,12 @@ def tile_maskedmultiheadattention_pa_kernel(
                 op=ALU.add,
             )
 
-        def sum_by_tensor(g, places):
-            for k in places:
-                if k >= 2:
+        def summed_heads(g):
+            return SUMMED_HEADS if g in SUMMED_BY_TENSOR else 0
+
+        def sum_by_tensor(g):
+            for k in range(SUMMED_HEADS):
+                if g == SUMMED_BY_TENSOR[1]:
                     head_sum = psum.tile([P, KEYS], F32, name="o_bank")
                 else:
                     head_sum = psum.tile([P, KEYS], F32, name="turned")
@@ -210,13 +213,12 @@ def tile_maskedmultiheadattention_pa_kernel(
 
         def row_maxima(g):
             top_of[g] = triple.tile([P, GROUP_SIZES[g]], F32, name="top")
-            if g in SUMMED_BY_TENSOR:
-                for k in range(GROUP_SIZES[g]):
-                    nc.vector.tensor_reduce(
-                        out=top_of[g][:, k : k + 1], in_=head_sums_of[g][k], axis=AXIS_X, op=ALU.max
-                    )
-                return
-            nc.vector.tensor_reduce(out=top_of[g][:], in_=sum_of[g][:], axis=AXIS_X, op=ALU.max)
+            summed = summed_heads(g)
+            for k in range(summed):
+                nc.vector.tensor_reduce(out=top_of[g][:, k : k + 1], in_=head_sums_of[g][k], axis=AXIS_X, op=ALU.max)
+            nc.vector.tensor_reduce(
+                out=top_of[g][:, summed:], in_=sum_of[g][:, summed:, :], axis=AXIS_X, op=ALU.max
+            )
 
         def exponentials(g, between):
             size = GROUP_SIZES[g]
@@ -224,7 +226,7 @@ def tile_maskedmultiheadattention_pa_kernel(
             if g == 0:
                 found_together = FIRST_LOADS
             elif g in SUMMED_BY_TENSOR:
-                found_together = [(k, k + 1) for k in range(size)]
+                found_together = [(k, k + 1) for k in range(SUMMED_HEADS)] + [(SUMMED_HEADS, size)]
             else:
                 found_together = ((0, size),)
             e = double.tile([P, size, KEYS], BF16, name="e")
@@ -251,8 +253,8 @@ def tile_maskedmultiheadattention_pa_kernel(
                     e_words = e[:, k, :].bitcast(F32)
                     for u in range(2):
                         nc.tensor.transpose(e_t[:, k - first, u, :], e_words[:, u : 2 * P : 2], identity[:])
-                if g + 1 in SUMMED_BY_TENSOR:
-                    sum_by_tensor(g + 1, pair)
+            if g + 2 in SUMMED_BY_TENSOR:
+                sum_by_tensor(g + 2)
             between()
             for first, e_t in turned:
                 pair = grouped_of[g][:, first * KEYS : min(first + 2, size) * KEYS].bitcast(F32)

@@ -40,12 +40,13 @@ LEADERS = range(1, GROUPS - 1, 2)
 BANK_HEADS = N_TILE // WIDTH
 BANKS = ALL_HEADS // BANK_HEADS
 LAST_GROUP = [max(g for g in range(GROUPS) if FIRST_HEAD[g] < (q + 1) * BANK_HEADS) for q in range(BANKS)]
-LOAD_BUFS = 5
+LOAD_BUFS = 6
 SUMMED_BY_TENSOR = (2, 3)
 SUMMED_HEADS = 2
 RUN = 4
 W_ROWS = FEATURES // P
-W_FIRST_STEP = 5
+W_LOAD_STEP = 4
+W_FIRST_STEP = 9
 W_PER_STEP = 2
 W_READY = W_FIRST_STEP + W_ROWS // W_PER_STEP
 
@@ -109,7 +110,7 @@ def tile_maskedmultiheadattention_pa_kernel(
         gain = const.tile([P, FEATURES], BF16)
         bias = const.tile([P, FEATURES], BF16)
 
-        head_sums_of, grouped_of, v_place_of = {}, {}, {}
+        head_sums_of, grouped_of, v_place_of, turned_of = {}, {}, {}, {}
         content_of, pos_of, v_raw_of, sum_of, top_of = {}, {}, {}, {}, {}
         e_codes_of, e_scales_of, v_grouped_of, ctx_bank_of = {}, {}, {}, {}
         w_grouped_of, c_of, c_words_of, c_grouped_of, c_codes_of, c_scales_of = {}, {}, {}, {}, {}, {}
@@ -124,7 +125,7 @@ def tile_maskedmultiheadattention_pa_kernel(
                 return columns
             share = GROUP_SIZES[g - 1] * 640 // 4
             if g - 3 in LAST_GROUP:
-                share += 512
+                share += 384
             return columns - min(columns - summed_heads(g) * KEYS, share)
 
         def load_scores(g):
@@ -220,7 +221,7 @@ def tile_maskedmultiheadattention_pa_kernel(
                 out=top_of[g][:, summed:], in_=sum_of[g][:, summed:, :], axis=AXIS_X, op=ALU.max
             )
 
-        def exponentials(g, between):
+        def exponentials(g):
             size = GROUP_SIZES[g]
             shift = double.tile([P, size], F32, name="shift")
             if g == 0:
@@ -244,19 +245,21 @@ def tile_maskedmultiheadattention_pa_kernel(
                 )
             if g not in grouped_of:
                 grouped_of[g] = double.tile([P, size * KEYS], BF16, name="e_grouped", align_bytes=64)
-            turned = []
+            turned_of[g] = []
             for first in range(0, size, 2):
                 pair = range(first, min(first + 2, size))
                 e_t = psum.tile([P, len(pair), 2, P], F32, name="e_t")
-                turned.append((first, e_t))
+                turned_of[g].append((first, e_t))
                 for k in pair:
                     e_words = e[:, k, :].bitcast(F32)
                     for u in range(2):
                         nc.tensor.transpose(e_t[:, k - first, u, :], e_words[:, u : 2 * P : 2], identity[:])
             if g + 2 in SUMMED_BY_TENSOR:
                 sum_by_tensor(g + 2)
-            between()
-            for first, e_t in turned:
+
+        def copy_exponentials(g):
+            size = GROUP_SIZES[g]
+            for first, e_t in turned_of[g]:
                 pair = grouped_of[g][:, first * KEYS : min(first + 2, size) * KEYS].bitcast(F32)
                 nc.scalar.copy(
                     out=pair.rearrange("p (k r u) -> p k r u", r=P, u=2), in_=e_t[:].rearrange("p k u r -> p k r u")
@@ -539,16 +542,17 @@ def tile_maskedmultiheadattention_pa_kernel(
                     quantise_c(b, (0,))
                 if step == LAST_GROUP[PASSES * b + 1] + 4:
                     quantise_c(b, (1,) if b == BATCH - 1 else (0, 1))
-            def regroup_now():
-                if 0 < step < GROUPS:
-                    regroup_values(step)
-
             if step == 0:
-                exponentials(0, lambda: regroup_values(0))
-            elif 0 < step - 1 < GROUPS:
-                exponentials(step - 1, regroup_now)
+                exponentials(0)
+                regroup_values(0)
+                copy_exponentials(0)
             else:
-                regroup_now()
+                if 0 < step - 1 < GROUPS:
+                    exponentials(step - 1)
+                if step < GROUPS:
+                    regroup_values(step)
+                if 0 < step - 1 < GROUPS:
+                    copy_exponentials(step - 1)
             for q in range(BANKS):
                 if step == LAST_GROUP[q] + 3:
                     turn_c(q)
@@ -575,12 +579,13 @@ def tile_maskedmultiheadattention_pa_kernel(
             if step + LOAD_BUFS < GROUPS:
                 load_scores(step + LOAD_BUFS)
                 load_values(step + LOAD_BUFS)
-            if step < 2:
-                rows = slice(step * W_ROWS // 2, (step + 1) * W_ROWS // 2)
+            if W_LOAD_STEP <= step < W_LOAD_STEP + 2:
+                half = step - W_LOAD_STEP
+                rows = slice(half * W_ROWS // 2, (half + 1) * W_ROWS // 2)
                 nc.sync.dma_start(out=w_raw[:, rows, :], in_=w_view[:, rows, :])
-            if step == 2:
+            if step == W_LOAD_STEP + 2:
                 nc.sync.dma_start(out=residual[:], in_=inputMHA)
-            if step == GROUPS - LOAD_BUFS:
+            if step == 11:
                 nc.sync.dma_start(out=gain[:], in_=ln_w.partition_broadcast(P))
                 nc.sync.dma_start(out=bias[:], in_=ln_b.partition_broadcast(P))
 

@@ -32,7 +32,7 @@ OPEN_KEYS = KEYS - WINDOW
 HIDDEN = 1e30
 
 GROUP_SIZES = 15 * (4,) + (2, 2)
-FIRST_LOADS = ((0, 1), (1, 2), (2, 4))
+FIRST_LOADS = ((0, 1), (1, 4))
 GROUPS = len(GROUP_SIZES)
 FIRST_HEAD = [sum(GROUP_SIZES[:g]) for g in range(GROUPS)]
 MAX_GROUP = 4
@@ -41,6 +41,7 @@ BANK_HEADS = N_TILE // WIDTH
 BANKS = ALL_HEADS // BANK_HEADS
 LAST_GROUP = [max(g for g in range(GROUPS) if FIRST_HEAD[g] < (q + 1) * BANK_HEADS) for q in range(BANKS)]
 LOAD_BUFS = 6
+RESIDUAL_STEPS = (13, 14, 15)
 SUMMED_BY_TENSOR = (2, 3)
 SUMMED_HEADS = 2
 RUN = 4
@@ -125,6 +126,8 @@ def tile_maskedmultiheadattention_pa_kernel(
                 return columns
             share = GROUP_SIZES[g - 1] * 640 // 4
             if g - 3 in LAST_GROUP:
+                share += 384
+            if g - 1 in RESIDUAL_STEPS:
                 share += 384
             return columns - min(columns - summed_heads(g) * KEYS, share)
 
@@ -441,10 +444,10 @@ def tile_maskedmultiheadattention_pa_kernel(
             moments = const.tile([P, 2], F32, name="moments")
             nc.vector.bn_aggr(out=moments[:], in_=stats[:].rearrange("p c k -> p (c k)"))
             mean_of[b] = moments[:, 0:1]
-            spread = double.tile([P, 1], F32, name="spread")
-            nc.scalar.activation(out=spread[:], in_=moments[:, 1:2], func=ACT.Identity, bias=eps[:])
             rstd_of[b] = const.tile([P, 1], F32, name="rstd_%d" % b)
-            nc.gpsimd.tensor_tensor(out=rstd_of[b][:], in0=spread[:], in1=minus_half[:], op=ALU.pow)
+            nc.scalar.activation(
+                out=rstd_of[b][:], in_=moments[:, 1:2], func=ACT.Abs_reciprocal_sqrt, bias=eps[:]
+            )
 
         def find_mean(b):
             total = double.tile([P, 1], F32, name="total")
@@ -467,11 +470,16 @@ def tile_maskedmultiheadattention_pa_kernel(
             nc.scalar.activation(
                 out=spread[:], in_=square_sum_of[b][:], func=ACT.Identity, scale=1.0 / FEATURES, bias=eps[:]
             )
+            rstd_of[b] = const.tile([P, 1], F32, name="rstd_%d" % b)
+            if b == BATCH - 2:
+                nc.scalar.activation(
+                    out=rstd_of[b][:], in_=mean_square[:], func=ACT.Abs_reciprocal_sqrt, scale=-1.0, bias=spread[:]
+                )
+                return
             spread_less = double.tile([P, 1], F32, name="spread_less")
             nc.scalar.activation(
                 out=spread_less[:], in_=mean_square[:], func=ACT.Identity, scale=-1.0, bias=spread[:]
             )
-            rstd_of[b] = const.tile([P, 1], F32, name="rstd_%d" % b)
             nc.gpsimd.tensor_tensor(out=rstd_of[b][:], in0=spread_less[:], in1=minus_half[:], op=ALU.pow)
 
         def layer_norm_parts(b):
@@ -523,7 +531,8 @@ def tile_maskedmultiheadattention_pa_kernel(
         def square_step(b):
             return project_step(PASSES * b + PASSES - 1) + (3 if b == BATCH - 2 else 1)
 
-        waiting = layer_norm_rows(0) + layer_norm_rows(1) + layer_norm_rows(2)
+        rows = [layer_norm_rows(b) for b in range(BATCH - 1)]
+        waiting = [rows[0][0], rows[1][0], rows[0][1], rows[1][1], rows[2][0], rows[2][1]]
 
         def use_wait(first, count):
             for part in waiting[first : first + count]:
@@ -564,6 +573,8 @@ def tile_maskedmultiheadattention_pa_kernel(
                     find_mean(b)
                 if step == square_step(b):
                     square(b)
+            if step == square_step(BATCH - 2):
+                nc.scalar.activation(out=table_warmer[:], in_=minus_half[:], func=ACT.Abs_reciprocal_sqrt)
             if W_FIRST_STEP <= step < W_READY:
                 turn_w(step - W_FIRST_STEP)
             if 0 <= ready < GROUPS:

@@ -33,6 +33,7 @@ HIDDEN = 1e30
 
 GROUP_SIZES = 15 * (4,) + (2, 2)
 FIRST_LOADS = ((0, 1), (1, 4))
+FIRST_STEPS = ((0, 1), (1, 4))
 GROUPS = len(GROUP_SIZES)
 FIRST_HEAD = [sum(GROUP_SIZES[:g]) for g in range(GROUPS)]
 MAX_GROUP = 4
@@ -111,6 +112,7 @@ def tile_maskedmultiheadattention_pa_kernel(
         gain = const.tile([P, FEATURES], BF16)
         bias = const.tile([P, FEATURES], BF16)
 
+        shift_of, e_of = {}, {}
         head_sums_of, grouped_of, v_place_of, turned_of = {}, {}, {}, {}
         content_of, pos_of, v_raw_of, sum_of, top_of = {}, {}, {}, {}, {}
         e_codes_of, e_scales_of, v_grouped_of, ctx_bank_of = {}, {}, {}, {}
@@ -175,7 +177,7 @@ def tile_maskedmultiheadattention_pa_kernel(
             sum_of[0] = triple.tile([P, GROUP_SIZES[0], KEYS], F32, name="score_sum")
             head_sums_of[0] = [sum_of[0][:, k, :] for k in range(GROUP_SIZES[0])]
             top_of[0] = triple.tile([P, GROUP_SIZES[0]], F32, name="top")
-            for start, end in FIRST_LOADS:
+            for start, end in FIRST_STEPS:
                 heads = slice(start, end)
                 window = pos_of[0][:, heads, OPEN_KEYS:KEYS]
                 nc.vector.tensor_tensor(
@@ -224,17 +226,20 @@ def tile_maskedmultiheadattention_pa_kernel(
                 out=top_of[g][:, summed:], in_=sum_of[g][:, summed:, :], axis=AXIS_X, op=ALU.max
             )
 
-        def exponentials(g):
+        def exponentials(g, places):
             size = GROUP_SIZES[g]
-            shift = double.tile([P, size], F32, name="shift")
+            if g not in e_of:
+                shift_of[g] = double.tile([P, size], F32, name="shift")
+                e_of[g] = double.tile([P, size, KEYS], BF16, name="e")
+            shift, e = shift_of[g], e_of[g]
             if g == 0:
-                found_together = FIRST_LOADS
+                found_together = FIRST_STEPS
             elif g in SUMMED_BY_TENSOR:
                 found_together = [(k, k + 1) for k in range(SUMMED_HEADS)] + [(SUMMED_HEADS, size)]
             else:
                 found_together = ((0, size),)
-            e = double.tile([P, size, KEYS], BF16, name="e")
-            for k, n in enumerate(heads_of(g)):
+            for k in places:
+                n = FIRST_HEAD[g] + k
                 for start, end in found_together:
                     if k == start:
                         nc.scalar.mul(out=shift[:, start:end], in_=top_of[g][:, start:end], mul=-SCALE)
@@ -246,6 +251,9 @@ def tile_maskedmultiheadattention_pa_kernel(
                     scale=SCALE,
                     accum_out=rowsum[:, n : n + 1],
                 )
+
+        def turn_exponentials(g):
+            size, e = GROUP_SIZES[g], e_of[g]
             if g not in grouped_of:
                 grouped_of[g] = double.tile([P, size * KEYS], BF16, name="e_grouped", align_bytes=64)
             turned_of[g] = []
@@ -279,12 +287,11 @@ def tile_maskedmultiheadattention_pa_kernel(
             else:
                 v_grouped_of[g] = double.tile([P, size * WIDTH * PACK], BF16, name="v_grouped", align_bytes=64)
                 home, start = v_grouped_of[g], 0
-            for k in range(size):
-                first = start + k * WIDTH * PACK
-                nc.scalar.copy(
-                    out=home[:, first : first + WIDTH * PACK].rearrange("p (c i t) -> p c t i", i=RUN, t=PACK),
-                    in_=v_raw_of[g][:, k, :, :].rearrange("p t (c i) -> p c t i", i=RUN),
-                )
+            whole = home[:, start : start + size * WIDTH * PACK]
+            nc.scalar.copy(
+                out=whole.rearrange("p (n c i t) -> p n c t i", n=size, i=RUN, t=PACK),
+                in_=v_raw_of[g][:].rearrange("p n t (c i) -> p n c t i", i=RUN),
+            )
 
         def quantise_group(g):
             size = GROUP_SIZES[g]
@@ -515,10 +522,10 @@ def tile_maskedmultiheadattention_pa_kernel(
             return [centre, finish]
 
         load_scores(0)
+        load_values(0)
         for g in range(1, LOAD_BUFS):
             load_scores(g)
-            load_values(g - 1)
-        load_values(LOAD_BUFS - 1)
+            load_values(g)
         first_group()
         make_hidden()
 
@@ -552,12 +559,15 @@ def tile_maskedmultiheadattention_pa_kernel(
                 if step == LAST_GROUP[PASSES * b + 1] + 4:
                     quantise_c(b, (1,) if b == BATCH - 1 else (0, 1))
             if step == 0:
-                exponentials(0)
+                exponentials(0, range(0, 1))
                 regroup_values(0)
+                exponentials(0, range(1, GROUP_SIZES[0]))
+                turn_exponentials(0)
                 copy_exponentials(0)
             else:
                 if 0 < step - 1 < GROUPS:
-                    exponentials(step - 1)
+                    exponentials(step - 1, range(GROUP_SIZES[step - 1]))
+                    turn_exponentials(step - 1)
                 if step < GROUPS:
                     regroup_values(step)
                 if 0 < step - 1 < GROUPS:

@@ -112,7 +112,8 @@ def tile_maskedmultiheadattention_pa_kernel(
         gain = const.tile([P, FEATURES], BF16)
         bias = const.tile([P, FEATURES], BF16)
 
-        shift_of, e_of = {}, {}
+        shift_of, e_of, v_home_of = {}, {}, {}
+        total_of, spread_of, mean_square_of = {}, {}, {}
         head_sums_of, grouped_of, v_place_of, turned_of = {}, {}, {}, {}
         content_of, pos_of, v_raw_of, sum_of, top_of = {}, {}, {}, {}, {}
         e_codes_of, e_scales_of, v_grouped_of, ctx_bank_of = {}, {}, {}, {}
@@ -128,7 +129,7 @@ def tile_maskedmultiheadattention_pa_kernel(
                 return columns
             share = GROUP_SIZES[g - 1] * 640 // 4
             if g - 3 in LAST_GROUP:
-                share += 384
+                share += 256
             if g - 1 in RESIDUAL_STEPS:
                 share += 384
             return columns - min(columns - summed_heads(g) * KEYS, share)
@@ -226,21 +227,20 @@ def tile_maskedmultiheadattention_pa_kernel(
                 out=top_of[g][:, summed:], in_=sum_of[g][:, summed:, :], axis=AXIS_X, op=ALU.max
             )
 
+        def find_shifts(g):
+            shift_of[g] = double.tile([P, GROUP_SIZES[g]], F32, name="shift")
+            nc.scalar.mul(out=shift_of[g][:], in_=top_of[g][:], mul=-SCALE)
+
         def exponentials(g, places):
             size = GROUP_SIZES[g]
             if g not in e_of:
-                shift_of[g] = double.tile([P, size], F32, name="shift")
                 e_of[g] = double.tile([P, size, KEYS], BF16, name="e")
-            shift, e = shift_of[g], e_of[g]
             if g == 0:
-                found_together = FIRST_STEPS
-            elif g in SUMMED_BY_TENSOR:
-                found_together = [(k, k + 1) for k in range(SUMMED_HEADS)] + [(SUMMED_HEADS, size)]
-            else:
-                found_together = ((0, size),)
+                shift_of[g] = shift_of.get(g) or double.tile([P, size], F32, name="shift")
+            shift, e = shift_of[g], e_of[g]
             for k in places:
                 n = FIRST_HEAD[g] + k
-                for start, end in found_together:
+                for start, end in FIRST_STEPS if g == 0 else ():
                     if k == start:
                         nc.scalar.mul(out=shift[:, start:end], in_=top_of[g][:, start:end], mul=-SCALE)
                 nc.scalar.activation(
@@ -276,21 +276,24 @@ def tile_maskedmultiheadattention_pa_kernel(
                     out=pair.rearrange("p (k r u) -> p k r u", r=P, u=2), in_=e_t[:].rearrange("p k u r -> p k r u")
                 )
 
-        def regroup_values(g):
+        def regroup_values(g, first, last):
             size = GROUP_SIZES[g]
-            if g in LEADERS:
+            if first > 0:
+                pass
+            elif g in LEADERS:
                 width = size * KEYS + (size + GROUP_SIZES[g + 1]) * WIDTH * PACK
                 grouped_of[g] = triple.tile([P, width], BF16, name="grouped", align_bytes=64)
-                home, start = grouped_of[g], size * KEYS
+                v_home_of[g] = grouped_of[g], size * KEYS
             elif g - 1 in LEADERS:
-                home, start = grouped_of[g - 1], GROUP_SIZES[g - 1] * (KEYS + WIDTH * PACK)
+                v_home_of[g] = grouped_of[g - 1], GROUP_SIZES[g - 1] * (KEYS + WIDTH * PACK)
             else:
                 v_grouped_of[g] = double.tile([P, size * WIDTH * PACK], BF16, name="v_grouped", align_bytes=64)
-                home, start = v_grouped_of[g], 0
-            whole = home[:, start : start + size * WIDTH * PACK]
+                v_home_of[g] = v_grouped_of[g], 0
+            home, start = v_home_of[g]
+            part = home[:, start + first * WIDTH * PACK : start + last * WIDTH * PACK]
             nc.scalar.copy(
-                out=whole.rearrange("p (n c i t) -> p n c t i", n=size, i=RUN, t=PACK),
-                in_=v_raw_of[g][:].rearrange("p n t (c i) -> p n c t i", i=RUN),
+                out=part.rearrange("p (n c i t) -> p n c t i", n=last - first, i=RUN, t=PACK),
+                in_=v_raw_of[g][:, first:last, :, :].rearrange("p n t (c i) -> p n c t i", i=RUN),
             )
 
         def quantise_group(g):
@@ -362,9 +365,9 @@ def tile_maskedmultiheadattention_pa_kernel(
                 op=ALU.mult,
             )
 
-        def transpose_words(rows, passes):
+        def transpose_words(rows, passes, banks):
             words = rows.bitcast(F32)
-            turned = psum.tile([P, passes * 2, P], F32, name="turned")
+            turned = psum.tile([P, passes * 2, P], F32, name=banks)
             for g in range(passes):
                 for u in range(2):
                     nc.tensor.transpose(
@@ -379,7 +382,7 @@ def tile_maskedmultiheadattention_pa_kernel(
             w_grouped_of[i] = double.tile([P, PASSES, W_PER_STEP * P, PACK], BF16, name="w_grouped", align_bytes=64)
             for r in range(W_PER_STEP):
                 copy_words(
-                    transpose_words(w_raw[:, i * W_PER_STEP + r, :], PASSES),
+                    transpose_words(w_raw[:, i * W_PER_STEP + r, :], PASSES, "o_bank"),
                     w_grouped_of[i][:, :, r * P : (r + 1) * P, :],
                 )
 
@@ -393,7 +396,7 @@ def tile_maskedmultiheadattention_pa_kernel(
                 )
 
         def turn_c(q):
-            c_words_of[q] = transpose_words(c_of[q][:].rearrange("p n i -> p (n i)"), 1)
+            c_words_of[q] = transpose_words(c_of[q][:].rearrange("p n i -> p (n i)"), 1, "turned")
 
         def copy_c(q):
             b, g = divmod(q, PASSES)
@@ -430,39 +433,51 @@ def tile_maskedmultiheadattention_pa_kernel(
 
         def add_residual(b):
             o_of[b] = const.tile([P, FEATURES], F32, name="o_%d" % b)
-            if b < BATCH - 1:
-                sums_of[b] = const.tile([P, HALVES], F32, name="sums_%d" % b)
-                for half in range(HALVES):
-                    outputs = slice(half * N_TILE, (half + 1) * N_TILE)
-                    nc.vector.scalar_tensor_tensor(
-                        out=o_of[b][:, outputs], in0=o_banks_of[b][half][:], scalar=1.0, in1=residual[:, b, outputs],
-                        op0=ALU.mult, op1=ALU.add, accum_out=sums_of[b][:, half : half + 1],
-                    )
-                return
-            stats = double.tile([P, HALVES, 6], F32, name="stats")
+            sums_of[b] = const.tile([P, HALVES], F32, name="sums_%d" % b)
             for half in range(HALVES):
                 outputs = slice(half * N_TILE, (half + 1) * N_TILE)
-                nc.vector.tensor_tensor(
-                    out=o_of[b][:, outputs], in0=o_banks_of[b][half][:], in1=residual[:, b, outputs], op=ALU.add
+                nc.vector.scalar_tensor_tensor(
+                    out=o_of[b][:, outputs], in0=o_banks_of[b][half][:], scalar=1.0, in1=residual[:, b, outputs],
+                    op0=ALU.mult, op1=ALU.add, accum_out=sums_of[b][:, half : half + 1],
                 )
+
+        def last_moments(b):
+            squares = double.tile([P, FEATURES], BF16, name="squares")
+            square_sums = const.tile([P, HALVES], F32, name="square_sums")
+            spreads = [const.tile([P, 1], F32, name="spread_%d" % half) for half in range(HALVES)]
             for half in range(HALVES):
                 outputs = slice(half * N_TILE, (half + 1) * N_TILE)
-                nc.vector.bn_stats(out=stats[:, half, :], in_=o_of[b][:, outputs])
-            moments = const.tile([P, 2], F32, name="moments")
-            nc.vector.bn_aggr(out=moments[:], in_=stats[:].rearrange("p c k -> p (c k)"))
-            mean_of[b] = moments[:, 0:1]
+                nc.scalar.activation(
+                    out=squares[:, outputs], in_=o_of[b][:, outputs], func=ACT.Square,
+                    accum_out=square_sums[:, half : half + 1],
+                )
+                if half == 0:
+                    before = eps[:]
+                    find_total(b)
+                else:
+                    before = spreads[half - 1][:]
+                    mean_square = double.tile([P, 1], F32, name="mean_square")
+                    nc.scalar.activation(out=mean_square[:], in_=mean_of[b], func=ACT.Square)
+                nc.scalar.activation(
+                    out=spreads[half][:], in_=square_sums[:, half : half + 1], func=ACT.Identity,
+                    scale=1.0 / FEATURES, bias=before,
+                )
+                if half == 0:
+                    find_mean(b)
             rstd_of[b] = const.tile([P, 1], F32, name="rstd_%d" % b)
             nc.scalar.activation(
-                out=rstd_of[b][:], in_=moments[:, 1:2], func=ACT.Abs_reciprocal_sqrt, bias=eps[:]
+                out=rstd_of[b][:], in_=mean_square[:], func=ACT.Abs_reciprocal_sqrt, scale=-1.0, bias=spreads[-1][:]
+            )
+
+        def find_total(b):
+            total_of[b] = double.tile([P, 1], F32, name="total")
+            nc.scalar.activation(
+                out=total_of[b][:], in_=sums_of[b][:, 0:1], func=ACT.Identity, bias=sums_of[b][:, 1:2]
             )
 
         def find_mean(b):
-            total = double.tile([P, 1], F32, name="total")
-            nc.scalar.activation(
-                out=total[:], in_=sums_of[b][:, 0:1], func=ACT.Identity, bias=sums_of[b][:, 1:2]
-            )
             mean = const.tile([P, 1], F32, name="mean_%d" % b)
-            nc.scalar.mul(out=mean[:], in_=total[:], mul=1.0 / FEATURES)
+            nc.scalar.mul(out=mean[:], in_=total_of[b][:], mul=1.0 / FEATURES)
             mean_of[b] = mean[:]
 
         def square(b):
@@ -470,13 +485,16 @@ def tile_maskedmultiheadattention_pa_kernel(
             square_sum_of[b] = const.tile([P, 1], F32, name="square_sum_%d" % b)
             nc.scalar.activation(out=squares[:], in_=o_of[b][:], func=ACT.Square, accum_out=square_sum_of[b][:])
 
-        def find_rstd(b):
-            mean_square = double.tile([P, 1], F32, name="mean_square")
-            nc.scalar.activation(out=mean_square[:], in_=mean_of[b], func=ACT.Square)
-            spread = double.tile([P, 1], F32, name="spread")
+        def find_spread(b):
+            spread_of[b] = double.tile([P, 1], F32, name="spread")
             nc.scalar.activation(
-                out=spread[:], in_=square_sum_of[b][:], func=ACT.Identity, scale=1.0 / FEATURES, bias=eps[:]
+                out=spread_of[b][:], in_=square_sum_of[b][:], func=ACT.Identity, scale=1.0 / FEATURES, bias=eps[:]
             )
+            mean_square_of[b] = double.tile([P, 1], F32, name="mean_square")
+            nc.scalar.activation(out=mean_square_of[b][:], in_=mean_of[b], func=ACT.Square)
+
+        def find_rstd(b):
+            spread, mean_square = spread_of[b], mean_square_of[b]
             rstd_of[b] = const.tile([P, 1], F32, name="rstd_%d" % b)
             if b == BATCH - 2:
                 nc.scalar.activation(
@@ -526,8 +544,8 @@ def tile_maskedmultiheadattention_pa_kernel(
         for g in range(1, LOAD_BUFS):
             load_scores(g)
             load_values(g)
-        first_group()
         make_hidden()
+        first_group()
 
         def project_step(q):
             b, g = divmod(q, PASSES)
@@ -549,6 +567,8 @@ def tile_maskedmultiheadattention_pa_kernel(
             ready = step - 2
             start, end = divided_heads(ready) if 0 <= ready < GROUPS else (0, 0)
 
+            if step == GROUPS:
+                use_wait(2, 1)
             if 0 < step < GROUPS:
                 add_scores(step)
             if W_FIRST_STEP < step <= W_READY:
@@ -558,44 +578,52 @@ def tile_maskedmultiheadattention_pa_kernel(
                     quantise_c(b, (0,))
                 if step == LAST_GROUP[PASSES * b + 1] + 4:
                     quantise_c(b, (1,) if b == BATCH - 1 else (0, 1))
+            for q in range(BANKS):
+                if step == LAST_GROUP[q] + 3:
+                    turn_c(q)
             if step == 0:
                 exponentials(0, range(0, 1))
-                regroup_values(0)
+                regroup_values(0, 0, GROUP_SIZES[0])
                 exponentials(0, range(1, GROUP_SIZES[0]))
                 turn_exponentials(0)
                 copy_exponentials(0)
             else:
                 if 0 < step - 1 < GROUPS:
+                    find_shifts(step - 1)
+                if step < GROUPS:
+                    regroup_values(step, 0, GROUP_SIZES[step] // 2)
+                if 0 < step - 1 < GROUPS:
                     exponentials(step - 1, range(GROUP_SIZES[step - 1]))
                     turn_exponentials(step - 1)
                 if step < GROUPS:
-                    regroup_values(step)
+                    regroup_values(step, GROUP_SIZES[step] // 2, GROUP_SIZES[step])
                 if 0 < step - 1 < GROUPS:
                     copy_exponentials(step - 1)
-            for q in range(BANKS):
-                if step == LAST_GROUP[q] + 3:
-                    turn_c(q)
             for q in range(BANKS):
                 if step == LAST_GROUP[q] + 3:
                     copy_c(q)
             for b in range(BATCH - 1):
                 if step == project_step(PASSES * b + PASSES - 1) + 1:
-                    find_mean(b)
+                    find_total(b)
                 if step == square_step(b):
                     square(b)
+                if step == (GROUPS if b == BATCH - 2 else square_step(b)):
+                    find_mean(b)
+                if step == square_step(b):
+                    find_spread(b)
             if step == square_step(BATCH - 2):
                 nc.scalar.activation(out=table_warmer[:], in_=minus_half[:], func=ACT.Abs_reciprocal_sqrt)
             if W_FIRST_STEP <= step < W_READY:
                 turn_w(step - W_FIRST_STEP)
             if 0 <= ready < GROUPS:
+                invert_rowsums(start, end)
                 quantise_group(ready)
                 attend(ready)
             for q in range(BANKS):
                 if step == project_step(q):
                     project(q)
             if step == GROUPS:
-                use_wait(2, 2)
-            invert_rowsums(start, end)
+                use_wait(3, 1)
 
             if step + LOAD_BUFS < GROUPS:
                 load_scores(step + LOAD_BUFS)
@@ -610,23 +638,24 @@ def tile_maskedmultiheadattention_pa_kernel(
                 nc.sync.dma_start(out=gain[:], in_=ln_w.partition_broadcast(P))
                 nc.sync.dma_start(out=bias[:], in_=ln_b.partition_broadcast(P))
 
-            if GROUPS - 2 <= step < GROUPS:
-                use_wait(step - (GROUPS - 2), 1)
-            if step == 1:
-                row_maxima(1)
+            if step == GROUPS - 2:
+                use_wait(0, 1)
+            if step == GROUPS - 1:
+                use_wait(1, 1)
             if step + 1 < GROUPS:
                 hide(step + 1)
-            if 1 < step < GROUPS:
+            if 0 < step < GROUPS:
                 row_maxima(step)
             divide(start, end)
             if step == GROUPS + 1:
                 use_wait(4, 1)
-            if step == GROUPS + 3:
-                use_wait(5, 1)
             for b in range(BATCH):
                 if step == project_step(PASSES * b + PASSES - 1):
                     add_residual(b)
+                    if b == BATCH - 1:
+                        last_moments(b)
                 if b < BATCH - 1 and step == square_step(b) + 1:
                     find_rstd(b)
+        use_wait(5, 1)
         for part in layer_norm_parts(BATCH - 1):
             part()

from contextlib import ExitStack

import concourse.mybir as mybir
from concourse.masks import make_identity

BF16 = mybir.dt.bfloat16
F32 = mybir.dt.float32
I32 = mybir.dt.int32
U32 = mybir.dt.uint32
U8 = mybir.dt.uint8
FP8X4 = mybir.dt.float8_e4m3fn_x4
ALU = mybir.AluOpType
ACT = mybir.ActivationFunctionType
AXIS_X = mybir.AxisListType.X

P = 128
BATCH = 4
HEADS = 16
KEYS = 512
WIDTH = 64
FEATURES = HEADS * WIDTH
ALL_HEADS = BATCH * HEADS
PACK = 4
K_PASS = P * PACK
PASSES = FEATURES // K_PASS
N_TILE = 512
HALVES = FEATURES // N_TILE
SCALE = 0.125
LN_EPS = 1e-5
WINDOW = P
OPEN_KEYS = KEYS - WINDOW
HIDDEN = 1e30

GROUP_SIZES = 15 * (4,) + (2, 2)
FIRST_LOADS = ((0, 1), (1, 4))
FIRST_STEPS = ((0, 1), (1, 4))
GROUPS = len(GROUP_SIZES)
FIRST_HEAD = [sum(GROUP_SIZES[:g]) for g in range(GROUPS)]
MAX_GROUP = 4
LEADERS = range(1, GROUPS - 1, 2)
BANK_HEADS = N_TILE // WIDTH
BANKS = ALL_HEADS // BANK_HEADS
LAST_GROUP = [max(g for g in range(GROUPS) if FIRST_HEAD[g] < (q + 1) * BANK_HEADS) for q in range(BANKS)]
LOAD_BUFS = 6
RESIDUAL_STEPS = (13, 14, 15)
SUMMED_BY_TENSOR = (2, 3)
SUMMED_HEADS = 2
RUN = 4
W_ROWS = FEATURES // P
W_LOAD_STEP = 4
W_FIRST_STEP = 9
W_PER_STEP = 2
W_READY = W_FIRST_STEP + W_ROWS // W_PER_STEP

FLOPS = 2 * ALL_HEADS * P * KEYS * WIDTH + 2 * BATCH * P * FEATURES * FEATURES


def tile_maskedmultiheadattention_pa_kernel(
    tc, content_scores, pos_scores, values, mask, inputMHA, W_out, ln_w, ln_b, out
):
    nc = tc.nc
    with ExitStack() as ctx:
        ctx.enter_context(tc.manual_schedule())
        const = ctx.enter_context(tc.tile_pool(name="const", bufs=1))
        loaded = ctx.enter_context(tc.tile_pool(name="loaded", bufs=LOAD_BUFS))
        triple = ctx.enter_context(tc.tile_pool(name="triple", bufs=3))
        double = ctx.enter_context(tc.tile_pool(name="double", bufs=2))
        psum = ctx.enter_context(tc.psum_pool(name="psum", bufs=2))

        content_view = content_scores.rearrange("b h s j -> s (b h) j")
        pos_flat = pos_scores.rearrange("b h s j -> (b h) (s j)")
        skew = KEYS - 1
        pos_from_0 = pos_flat[:, P - 1 : P - 1 + P * skew].rearrange("n (s j) -> s n j", j=skew)
        pos_from_1 = pos_flat[:, P : P + P * skew].rearrange("n (s j) -> s n j", j=skew)
        values_view = values.rearrange("b h (p t) i -> p (b h) (t i)", t=PACK)
        w_view = W_out.rearrange("(r p) f -> p r f", p=P)

        mask_words = const.tile([P, WINDOW, 2], I32)
        nc.sync.dma_start(
            out=mask_words[:].rearrange("p j w -> p (j w)"), in_=mask.bitcast(I32)[:, 2 * OPEN_KEYS : 2 * KEYS]
        )
        identity = const.tile([P, P], F32)
        make_identity(nc, identity[:])
        identity_bf16 = const.tile([P, P], BF16)
        make_identity(nc, identity_bf16[:])
        minus_half = const.tile([P, 1], F32)
        nc.vector.memset(minus_half[:], -0.5)
        eps = const.tile([P, 1], F32)
        nc.vector.tensor_scalar(
            out=eps[:], in0=minus_half[:], scalar1=0.0, scalar2=LN_EPS, op0=ALU.mult, op1=ALU.add
        )
        table_warmer = const.tile([P, 1], F32)
        nc.scalar.activation(out=table_warmer[:], in_=minus_half[:], func=ACT.Exp)
        cap = const.tile([P, WINDOW], BF16)
        nc.vector.tensor_scalar(
            out=cap[:], in0=mask_words[:, :, 0], scalar1=-2.0 * HIDDEN, scalar2=HIDDEN, op0=ALU.mult, op1=ALU.add
        )

        hidden = const.tile([P, WINDOW], BF16)

        def make_hidden():
            nc.vector.tensor_scalar(
                out=hidden[:], in0=mask_words[:, :, 0], scalar1=-HIDDEN, scalar2=0.0, op0=ALU.mult, op1=ALU.add
            )

        rowsum = const.tile([P, ALL_HEADS], F32)
        inverse = const.tile([P, ALL_HEADS], F32)
        w_raw = const.tile([P, W_ROWS, FEATURES], BF16)
        w_codes = const.tile([P, PASSES, FEATURES], U32, align_bytes=64)
        w_scales = const.tile([P, PASSES, FEATURES], U8, align_bytes=64)
        residual = const.tile([P, BATCH, FEATURES], BF16)
        gain = const.tile([P, FEATURES], BF16)
        bias = const.tile([P, FEATURES], BF16)

        shift_of, e_of, v_home_of = {}, {}, {}
        total_of, spread_of, mean_square_of = {}, {}, {}
        head_sums_of, grouped_of, v_place_of, turned_of = {}, {}, {}, {}
        content_of, pos_of, v_raw_of, sum_of, top_of = {}, {}, {}, {}, {}
        e_codes_of, e_scales_of, v_grouped_of, ctx_bank_of = {}, {}, {}, {}
        w_grouped_of, c_of, c_words_of, c_grouped_of, c_codes_of, c_scales_of = {}, {}, {}, {}, {}, {}
        o_banks_of, o_of, mean_of, rstd_of, sums_of, square_sum_of = {}, {}, {}, {}, {}, {}

        def heads_of(g):
            return range(FIRST_HEAD[g], FIRST_HEAD[g] + GROUP_SIZES[g])

        def vector_columns(g):
            columns = GROUP_SIZES[g] * KEYS
            if g < 3:
                return columns
            share = GROUP_SIZES[g - 1] * 640 // 4
            if g - 3 in LAST_GROUP:
                share += 256
            if g - 1 in RESIDUAL_STEPS:
                share += 384
            return columns - min(columns - summed_heads(g) * KEYS, share)

        def load_scores(g):
            n, size = FIRST_HEAD[g], GROUP_SIZES[g]
            pos_of[g] = loaded.tile([P, size, KEYS], BF16, name="pos")
            content_of[g] = loaded.tile([P, size, KEYS], BF16, name="content")
            for start, end in FIRST_LOADS if g == 0 else ((0, size),):
                places, heads = slice(start, end), slice(n + start, n + end)
                window = pos_of[g][:, places, OPEN_KEYS:KEYS]
                nc.sync.dma_start(out=window, in_=pos_from_1[:, heads, OPEN_KEYS - 1 : KEYS - 1])
                nc.sync.dma_start(out=pos_of[g][:, places, 0:OPEN_KEYS], in_=pos_from_0[:, heads, 0:OPEN_KEYS])
                nc.sync.dma_start(out=content_of[g][:, places, :], in_=content_view[:, heads, :])

        def load_values(g):
            n, size = FIRST_HEAD[g], GROUP_SIZES[g]
            v_raw_of[g] = loaded.tile([P, size, PACK, WIDTH], BF16, name="v_raw")
            nc.sync.dma_start(
                out=v_raw_of[g][:].rearrange("p n t i -> p n (t i)"), in_=values_view[:, n : n + size, :]
            )

        def flat(tile):
            return tile[:].rearrange("p n j -> p (n j)")

        def hide(g):
            size, summed = GROUP_SIZES[g], summed_heads(g)
            window = pos_of[g][:, summed:size, OPEN_KEYS:KEYS]
            nc.vector.tensor_tensor(
                out=window, in0=window, in1=cap[:].unsqueeze(1).to_broadcast([P, size - summed, WINDOW]), op=ALU.min
            )
            sum_of[g] = triple.tile([P, size, KEYS], F32, name="score_sum")
            for k in range(summed, size):
                head_sums_of.setdefault(g, []).append(sum_of[g][:, k, :])
            first = vector_columns(g)
            if first < size * KEYS:
                columns = slice(first, size * KEYS)
                nc.gpsimd.tensor_tensor(
                    out=flat(sum_of[g])[:, columns],
                    in0=flat(content_of[g])[:, columns],
                    in1=flat(pos_of[g])[:, columns],
                    op=ALU.add,
                )

        def first_group():
            sum_of[0] = triple.tile([P, GROUP_SIZES[0], KEYS], F32, name="score_sum")
            head_sums_of[0] = [sum_of[0][:, k, :] for k in range(GROUP_SIZES[0])]
            top_of[0] = triple.tile([P, GROUP_SIZES[0]], F32, name="top")
            for start, end in FIRST_STEPS:
                heads = slice(start, end)
                window = pos_of[0][:, heads, OPEN_KEYS:KEYS]
                nc.vector.tensor_tensor(
                    out=window, in0=window, in1=cap[:].unsqueeze(1).to_broadcast([P, end - start, WINDOW]), op=ALU.min
                )
                nc.vector.tensor_tensor(
                    out=sum_of[0][:, heads, :], in0=content_of[0][:, heads, :], in1=pos_of[0][:, heads, :], op=ALU.add
                )
                nc.vector.tensor_reduce(out=top_of[0][:, heads], in_=sum_of[0][:, heads, :], axis=AXIS_X, op=ALU.max)

        def add_scores(g):
            columns = slice(summed_heads(g) * KEYS, vector_columns(g))
            if columns.start == columns.stop:
                return
            nc.vector.tensor_tensor(
                out=flat(sum_of[g])[:, columns],
                in0=flat(content_of[g])[:, columns],
                in1=flat(pos_of[g])[:, columns],
                op=ALU.add,
            )

        def summed_heads(g):
            return SUMMED_HEADS if g in SUMMED_BY_TENSOR else 0

        def sum_by_tensor(g):
            for k in range(SUMMED_HEADS):
                if g == SUMMED_BY_TENSOR[1]:
                    head_sum = psum.tile([P, KEYS], F32, name="o_bank")
                else:
                    head_sum = psum.tile([P, KEYS], F32, name="turned")
                nc.tensor.matmul(
                    head_sum[:], lhsT=identity_bf16[:], rhs=content_of[g][:, k, :], start=True, stop=False
                )
                nc.tensor.matmul(
                    head_sum[:, OPEN_KEYS:KEYS], lhsT=identity_bf16[:], rhs=hidden[:], start=False, stop=False
                )
                nc.tensor.matmul(head_sum[:], lhsT=identity_bf16[:], rhs=pos_of[g][:, k, :], start=False, stop=True)
                head_sums_of.setdefault(g, []).append(head_sum[:])

        def row_maxima(g):
            top_of[g] = triple.tile([P, GROUP_SIZES[g]], F32, name="top")
            summed = summed_heads(g)
            for k in range(summed):
                nc.vector.tensor_reduce(out=top_of[g][:, k : k + 1], in_=head_sums_of[g][k], axis=AXIS_X, op=ALU.max)
            nc.vector.tensor_reduce(
                out=top_of[g][:, summed:], in_=sum_of[g][:, summed:, :], axis=AXIS_X, op=ALU.max
            )

        def find_shifts(g):
            shift_of[g] = double.tile([P, GROUP_SIZES[g]], F32, name="shift")
            nc.scalar.mul(out=shift_of[g][:], in_=top_of[g][:], mul=-SCALE)

        def exponentials(g, places):
            size = GROUP_SIZES[g]
            if g not in e_of:
                e_of[g] = double.tile([P, size, KEYS], BF16, name="e")
            if g == 0:
                shift_of[g] = shift_of.get(g) or double.tile([P, size], F32, name="shift")
            shift, e = shift_of[g], e_of[g]
            for k in places:
                n = FIRST_HEAD[g] + k
                for start, end in FIRST_STEPS if g == 0 else ():
                    if k == start:
                        nc.scalar.mul(out=shift[:, start:end], in_=top_of[g][:, start:end], mul=-SCALE)
                nc.scalar.activation(
                    out=e[:, k, :],
                    in_=head_sums_of[g][k],
                    func=ACT.Exp,
                    bias=shift[:, k : k + 1],
                    scale=SCALE,
                    accum_out=rowsum[:, n : n + 1],
                )

        def turn_exponentials(g):
            size, e = GROUP_SIZES[g], e_of[g]
            if g not in grouped_of:
                grouped_of[g] = double.tile([P, size * KEYS], BF16, name="e_grouped", align_bytes=64)
            turned_of[g] = []
            for first in range(0, size, 2):
                pair = range(first, min(first + 2, size))
                e_t = psum.tile([P, len(pair), 2, P], F32, name="e_t")
                turned_of[g].append((first, e_t))
                for k in pair:
                    e_words = e[:, k, :].bitcast(F32)
                    for u in range(2):
                        nc.tensor.transpose(e_t[:, k - first, u, :], e_words[:, u : 2 * P : 2], identity[:])
            if g + 2 in SUMMED_BY_TENSOR:
                sum_by_tensor(g + 2)

        def copy_exponentials(g):
            size = GROUP_SIZES[g]
            for first, e_t in turned_of[g]:
                pair = grouped_of[g][:, first * KEYS : min(first + 2, size) * KEYS].bitcast(F32)
                nc.scalar.copy(
                    out=pair.rearrange("p (k r u) -> p k r u", r=P, u=2), in_=e_t[:].rearrange("p k u r -> p k r u")
                )

        def regroup_values(g, first, last):
            size = GROUP_SIZES[g]
            if first > 0:
                pass
            elif g in LEADERS:
                width = size * KEYS + (size + GROUP_SIZES[g + 1]) * WIDTH * PACK
                grouped_of[g] = triple.tile([P, width], BF16, name="grouped", align_bytes=64)
                v_home_of[g] = grouped_of[g], size * KEYS
            elif g - 1 in LEADERS:
                v_home_of[g] = grouped_of[g - 1], GROUP_SIZES[g - 1] * (KEYS + WIDTH * PACK)
            else:
                v_grouped_of[g] = double.tile([P, size * WIDTH * PACK], BF16, name="v_grouped", align_bytes=64)
                v_home_of[g] = v_grouped_of[g], 0
            home, start = v_home_of[g]
            part = home[:, start + first * WIDTH * PACK : start + last * WIDTH * PACK]
            nc.scalar.copy(
                out=part.rearrange("p (n c i t) -> p n c t i", n=last - first, i=RUN, t=PACK),
                in_=v_raw_of[g][:, first:last, :, :].rearrange("p n t (c i) -> p n c t i", i=RUN),
            )

        def quantise_group(g):
            size = GROUP_SIZES[g]
            width = size * P
            if g in LEADERS:
                width += (size + GROUP_SIZES[g + 1]) * WIDTH
                codes = double.tile([P, width], U32, name="codes", align_bytes=64)
                scales = double.tile([P, width], U8, name="scales", align_bytes=64)
                for n in heads_of(g):
                    v_place_of[n] = codes, scales, size * P + (n - FIRST_HEAD[g]) * WIDTH
                for n in heads_of(g + 1):
                    v_place_of[n] = codes, scales, size * P + (n - FIRST_HEAD[g]) * WIDTH
            else:
                codes = double.tile([P, width], U32, name="e_codes", align_bytes=64)
                scales = double.tile([P, width], U8, name="e_scales", align_bytes=64)
            e_codes_of[g], e_scales_of[g] = codes, scales
            nc.vector.quantize_mx(out=codes[:].bitcast(FP8X4), scales=scales[:], in_=grouped_of[g][:])
            if g in v_grouped_of:
                codes = double.tile([P, size * WIDTH], U32, name="v_codes", align_bytes=64)
                scales = double.tile([P, size * WIDTH], U8, name="v_scales", align_bytes=64)
                for n in heads_of(g):
                    v_place_of[n] = codes, scales, (n - FIRST_HEAD[g]) * WIDTH
                nc.vector.quantize_mx(out=codes[:].bitcast(FP8X4), scales=scales[:], in_=v_grouped_of[g][:])

        def attend(g):
            for k, n in enumerate(heads_of(g)):
                bank, place = divmod(n, BANK_HEADS)
                if place == 0:
                    ctx_bank_of[bank] = psum.tile([P, BANK_HEADS, WIDTH], F32, name="ctx_bank")
                queries = slice(k * P, (k + 1) * P)
                v_codes, v_scales, first = v_place_of[n]
                features = slice(first, first + WIDTH)
                nc.tensor.matmul_mx(
                    out=ctx_bank_of[bank][:, place, :],
                    lhsT=e_codes_of[g][:, queries].bitcast(FP8X4),
                    lhsT_scale=e_scales_of[g][:, queries],
                    rhs=v_codes[:, features].bitcast(FP8X4),
                    rhs_scale=v_scales[:, features],
                    start=True,
                    stop=True,
                )

        def divided_heads(g):
            end = FIRST_HEAD[g] + GROUP_SIZES[g]
            if g == GROUPS - 1:
                return FIRST_HEAD[g], end
            if g == GROUPS - 2:
                return FIRST_HEAD[LAST_GROUP[BANKS - 2] + 1], end
            if g in LAST_GROUP:
                return end - BANK_HEADS, end
            return end, end

        def invert_rowsums(start, end):
            if start < end:
                nc.vector.reciprocal(out=inverse[:, start:end], in_=rowsum[:, start:end])

        def divide(start, end):
            if start == end:
                return
            bank, first = divmod(start, BANK_HEADS)
            size = end - start
            if first == 0:
                c_of[bank] = double.tile([P, BANK_HEADS, WIDTH], BF16, name="c")
            nc.vector.tensor_tensor(
                out=c_of[bank][:, first : first + size, :],
                in0=ctx_bank_of[bank][:, first : first + size, :],
                in1=inverse[:, start:end].unsqueeze(2).to_broadcast([P, size, WIDTH]),
                op=ALU.mult,
            )

        def transpose_words(rows, passes, banks):
            words = rows.bitcast(F32)
            turned = psum.tile([P, passes * 2, P], F32, name=banks)
            for g in range(passes):
                for u in range(2):
                    nc.tensor.transpose(
                        turned[:, 2 * g + u, :], words[:, 2 * P * g + u : 2 * P * (g + 1) : 2], identity[:]
                    )
            return turned

        def copy_words(turned, grouped):
            nc.scalar.copy(out=grouped.bitcast(F32), in_=turned[:].rearrange("p (g u) r -> p g r u", u=2))

        def turn_w(i):
            w_grouped_of[i] = double.tile([P, PASSES, W_PER_STEP * P, PACK], BF16, name="w_grouped", align_bytes=64)
            for r in range(W_PER_STEP):
                copy_words(
                    transpose_words(w_raw[:, i * W_PER_STEP + r, :], PASSES, "o_bank"),
                    w_grouped_of[i][:, :, r * P : (r + 1) * P, :],
                )

        def quantise_w(i):
            rows = slice(i * W_PER_STEP * P, (i + 1) * W_PER_STEP * P)
            for g in range(PASSES):
                nc.vector.quantize_mx(
                    out=w_codes[:, g, rows].bitcast(FP8X4),
                    scales=w_scales[:, g, rows],
                    in_=w_grouped_of[i][:, g, :, :].rearrange("p r t -> p (r t)"),
                )

        def turn_c(q):
            c_words_of[q] = transpose_words(c_of[q][:].rearrange("p n i -> p (n i)"), 1, "turned")

        def copy_c(q):
            b, g = divmod(q, PASSES)
            if g == 0:
                c_grouped_of[b] = double.tile([P, PASSES, P, PACK], BF16, name="c_grouped", align_bytes=64)
                c_codes_of[b] = double.tile([P, PASSES * P], U32, name="c_codes", align_bytes=64)
                c_scales_of[b] = double.tile([P, PASSES * P], U8, name="c_scales", align_bytes=64)
            copy_words(c_words_of[q], c_grouped_of[b][:, g : g + 1, :, :])

        def quantise_c(b, passes):
            columns = slice(passes[0] * P, (passes[-1] + 1) * P)
            nc.vector.quantize_mx(
                out=c_codes_of[b][:, columns].bitcast(FP8X4),
                scales=c_scales_of[b][:, columns],
                in_=c_grouped_of[b][:, passes[0] : passes[-1] + 1, :, :].rearrange("p g s t -> p (g s t)"),
            )

        def project(q):
            b, g = divmod(q, PASSES)
            queries = slice(g * P, (g + 1) * P)
            if g == 0:
                o_banks_of[b] = [psum.tile([P, N_TILE], F32, name="o_bank") for half in range(HALVES)]
            for half in range(HALVES):
                outputs = slice(half * N_TILE, (half + 1) * N_TILE)
                nc.tensor.matmul_mx(
                    out=o_banks_of[b][half][:],
                    lhsT=c_codes_of[b][:, queries].bitcast(FP8X4),
                    lhsT_scale=c_scales_of[b][:, queries],
                    rhs=w_codes[:, g, outputs].bitcast(FP8X4),
                    rhs_scale=w_scales[:, g, outputs],
                    start=(g == 0),
                    stop=(g == PASSES - 1),
                )

        def add_residual(b):
            o_of[b] = const.tile([P, FEATURES], F32, name="o_%d" % b)
            sums_of[b] = const.tile([P, HALVES], F32, name="sums_%d" % b)
            for half in range(HALVES):
                outputs = slice(half * N_TILE, (half + 1) * N_TILE)
                nc.vector.scalar_tensor_tensor(
                    out=o_of[b][:, outputs], in0=o_banks_of[b][half][:], scalar=1.0, in1=residual[:, b, outputs],
                    op0=ALU.mult, op1=ALU.add, accum_out=sums_of[b][:, half : half + 1],
                )

        def last_moments(b):
            squares = double.tile([P, FEATURES], BF16, name="squares")
            square_sums = const.tile([P, HALVES], F32, name="square_sums")
            spreads = [const.tile([P, 1], F32, name="spread_%d" % half) for half in range(HALVES)]
            for half in range(HALVES):
                outputs = slice(half * N_TILE, (half + 1) * N_TILE)
                nc.scalar.activation(
                    out=squares[:, outputs], in_=o_of[b][:, outputs], func=ACT.Square,
                    accum_out=square_sums[:, half : half + 1],
                )
                if half == 0:
                    before = eps[:]
                    find_total(b)
                else:
                    before = spreads[half - 1][:]
                    mean_square = double.tile([P, 1], F32, name="mean_square")
                    nc.scalar.activation(out=mean_square[:], in_=mean_of[b], func=ACT.Square)
                nc.scalar.activation(
                    out=spreads[half][:], in_=square_sums[:, half : half + 1], func=ACT.Identity,
                    scale=1.0 / FEATURES, bias=before,
                )
                if half == 0:
                    find_mean(b)
            rstd_of[b] = const.tile([P, 1], F32, name="rstd_%d" % b)
            nc.scalar.activation(
                out=rstd_of[b][:], in_=mean_square[:], func=ACT.Abs_reciprocal_sqrt, scale=-1.0, bias=spreads[-1][:]
            )

        def find_total(b):
            total_of[b] = double.tile([P, 1], F32, name="total")
            nc.scalar.activation(
                out=total_of[b][:], in_=sums_of[b][:, 0:1], func=ACT.Identity, bias=sums_of[b][:, 1:2]
            )

        def find_mean(b):
            mean = const.tile([P, 1], F32, name="mean_%d" % b)
            nc.scalar.mul(out=mean[:], in_=total_of[b][:], mul=1.0 / FEATURES)
            mean_of[b] = mean[:]

        def square(b):
            squares = double.tile([P, FEATURES], BF16, name="squares")
            square_sum_of[b] = const.tile([P, 1], F32, name="square_sum_%d" % b)
            nc.scalar.activation(out=squares[:], in_=o_of[b][:], func=ACT.Square, accum_out=square_sum_of[b][:])

        def find_spread(b):
            spread_of[b] = double.tile([P, 1], F32, name="spread")
            nc.scalar.activation(
                out=spread_of[b][:], in_=square_sum_of[b][:], func=ACT.Identity, scale=1.0 / FEATURES, bias=eps[:]
            )
            mean_square_of[b] = double.tile([P, 1], F32, name="mean_square")
            nc.scalar.activation(out=mean_square_of[b][:], in_=mean_of[b], func=ACT.Square)

        def find_rstd(b):
            spread, mean_square = spread_of[b], mean_square_of[b]
            rstd_of[b] = const.tile([P, 1], F32, name="rstd_%d" % b)
            if b == BATCH - 2:
                nc.scalar.activation(
                    out=rstd_of[b][:], in_=mean_square[:], func=ACT.Abs_reciprocal_sqrt, scale=-1.0, bias=spread[:]
                )
                return
            spread_less = double.tile([P, 1], F32, name="spread_less")
            nc.scalar.activation(
                out=spread_less[:], in_=mean_square[:], func=ACT.Identity, scale=-1.0, bias=spread[:]
            )
            nc.gpsimd.tensor_tensor(out=rstd_of[b][:], in0=spread_less[:], in1=minus_half[:], op=ALU.pow)

        def layer_norm_parts(b):
            def centre(half):
                outputs = slice(half * N_TILE, (half + 1) * N_TILE)
                nc.vector.scalar_tensor_tensor(
                    out=o_of[b][:, outputs], in0=o_of[b][:, outputs], scalar=mean_of[b],
                    in1=gain[:, outputs], op0=ALU.subtract, op1=ALU.mult,
                )

            def finish(half):
                outputs = slice(half * N_TILE, (half + 1) * N_TILE)
                nc.vector.scalar_tensor_tensor(
                    out=o_of[b][:, outputs], in0=o_of[b][:, outputs], scalar=rstd_of[b][:, 0:1],
                    in1=bias[:, outputs], op0=ALU.mult, op1=ALU.add,
                )
                nc.sync.dma_start(out=out[:, b, outputs], in_=o_of[b][:, outputs])

            return [lambda: centre(0), lambda: centre(1), lambda: finish(0), lambda: finish(1)]

        def layer_norm_rows(b):
            def centre():
                nc.vector.scalar_tensor_tensor(
                    out=o_of[b][:], in0=o_of[b][:], scalar=mean_of[b], in1=gain[:], op0=ALU.subtract, op1=ALU.mult
                )

            def finish():
                nc.vector.scalar_tensor_tensor(
                    out=o_of[b][:], in0=o_of[b][:], scalar=rstd_of[b][:, 0:1], in1=bias[:], op0=ALU.mult, op1=ALU.add
                )
                nc.sync.dma_start(out=out[:, b, :], in_=o_of[b][:])

            return [centre, finish]

        load_scores(0)
        load_values(0)
        for g in range(1, LOAD_BUFS):
            load_scores(g)
            load_values(g)
        make_hidden()
        first_group()

        def project_step(q):
            b, g = divmod(q, PASSES)
            if b < BATCH - 1:
                return max(LAST_GROUP[PASSES * b + 1] + 4, W_READY + b)
            return LAST_GROUP[q] + 4

        def square_step(b):
            return project_step(PASSES * b + PASSES - 1) + (3 if b == BATCH - 2 else 1)

        rows = [layer_norm_rows(b) for b in range(BATCH - 1)]
        waiting = [rows[0][0], rows[1][0], rows[0][1], rows[1][1], rows[2][0], rows[2][1]]

        def use_wait(first, count):
            for part in waiting[first : first + count]:
                part()

        for step in range(GROUPS + 4):
            ready = step - 2
            start, end = divided_heads(ready) if 0 <= ready < GROUPS else (0, 0)

            if step == GROUPS:
                use_wait(2, 1)
            if 0 < step < GROUPS:
                add_scores(step)
            if W_FIRST_STEP < step <= W_READY:
                quantise_w(step - W_FIRST_STEP - 1)
            for b in range(BATCH):
                if b == BATCH - 1 and step == LAST_GROUP[PASSES * b] + 4:
                    quantise_c(b, (0,))
                if step == LAST_GROUP[PASSES * b + 1] + 4:
                    quantise_c(b, (1,) if b == BATCH - 1 else (0, 1))
            for q in range(BANKS):
                if step == LAST_GROUP[q] + 3:
                    turn_c(q)
            if step == 0:
                exponentials(0, range(0, 1))
                regroup_values(0, 0, GROUP_SIZES[0])
                exponentials(0, range(1, GROUP_SIZES[0]))
                turn_exponentials(0)
                copy_exponentials(0)
            else:
                if 0 < step - 1 < GROUPS:
                    find_shifts(step - 1)
                if step < GROUPS:
                    regroup_values(step, 0, GROUP_SIZES[step] // 2)
                if 0 < step - 1 < GROUPS:
                    exponentials(step - 1, range(GROUP_SIZES[step - 1]))
                    turn_exponentials(step - 1)
                if step < GROUPS:
                    regroup_values(step, GROUP_SIZES[step] // 2, GROUP_SIZES[step])
                if 0 < step - 1 < GROUPS:
                    copy_exponentials(step - 1)
            for q in range(BANKS):
                if step == LAST_GROUP[q] + 3:
                    copy_c(q)
            for b in range(BATCH - 1):
                if step == project_step(PASSES * b + PASSES - 1) + 1:
                    find_total(b)
                if step == square_step(b):
                    square(b)
                if step == (GROUPS if b == BATCH - 2 else square_step(b)):
                    find_mean(b)
                if step == square_step(b):
                    find_spread(b)
            if step == square_step(BATCH - 2):
                nc.scalar.activation(out=table_warmer[:], in_=minus_half[:], func=ACT.Abs_reciprocal_sqrt)
            if W_FIRST_STEP <= step < W_READY:
                turn_w(step - W_FIRST_STEP)
            if 0 <= ready < GROUPS:
                invert_rowsums(start, end)
                quantise_group(ready)
                attend(ready)
            for q in range(BANKS):
                if step == project_step(q):
                    project(q)
            if step == GROUPS:
                use_wait(3, 1)

            if step + LOAD_BUFS < GROUPS:
                load_scores(step + LOAD_BUFS)
                load_values(step + LOAD_BUFS)
            if W_LOAD_STEP <= step < W_LOAD_STEP + 2:
                half = step - W_LOAD_STEP
                rows = slice(half * W_ROWS // 2, (half + 1) * W_ROWS // 2)
                nc.sync.dma_start(out=w_raw[:, rows, :], in_=w_view[:, rows, :])
            if step == W_LOAD_STEP + 2:
                nc.sync.dma_start(out=residual[:], in_=inputMHA)
            if step == 11:
                nc.sync.dma_start(out=gain[:], in_=ln_w.partition_broadcast(P))
                nc.sync.dma_start(out=bias[:], in_=ln_b.partition_broadcast(P))

            if step == GROUPS - 2:
                use_wait(0, 1)
            if step == GROUPS - 1:
                use_wait(1, 1)
            if step + 1 < GROUPS:
                hide(step + 1)
            if 0 < step < GROUPS:
                row_maxima(step)
            divide(start, end)
            if step == GROUPS + 1:
                use_wait(4, 1)
            for b in range(BATCH):
                if step == project_step(PASSES * b + PASSES - 1):
                    add_residual(b)
                    if b == BATCH - 1:
                        last_moments(b)
                if b < BATCH - 1 and step == square_step(b) + 1:
                    find_rstd(b)
        use_wait(5, 1)
        for part in layer_norm_parts(BATCH - 1):
            part()
